import numpy as np
import ml_dtypes


def mxq(x, axis, fmt="e4m3"):
    dtype, down = {"e4m3": (ml_dtypes.float8_e4m3fn, 7), "e5m2": (ml_dtypes.float8_e5m2, 14)}[fmt]
    v = np.moveaxis(np.asarray(x, np.float32).astype(ml_dtypes.bfloat16).astype(np.float64), axis, -1)
    blocks = v.reshape(v.shape[:-1] + (-1, 32))
    amax = np.abs(blocks).max(-1, keepdims=True)
    byte = np.maximum(np.where(amax > 0, np.frexp(amax)[1] - 1 + 127, 0) - down, 1)
    scale = np.exp2(byte - 127.0)
    codes = (blocks / scale).astype(np.float32).astype(dtype).astype(np.float64)
    return np.moveaxis((codes * scale).reshape(v.shape), -1, axis)


WIDE = False


def mx_kscale(k):
    if not WIDE:
        return np.ones(k)
    levels = np.array([10, -10, 5, -5, 0])
    a = np.random.permutation(np.resize(levels, k // 512 * 4)).reshape(k // 512, 4)
    idx = np.arange(k)
    return np.exp2(a[idx // 512, idx % 128 // 32])


BF16 = ml_dtypes.bfloat16


def bf(x):
    return np.asarray(x, np.float32).astype(BF16)


def f64(x):
    return np.asarray(x).astype(np.float64)


B, S, D, H, QL, KVL, NOPE, ROPE, VD = 4, 1024, 512, 2, 1536, 512, 128, 128, 128
HALF = ROPE // 2
ROPE_BASE = 10000.0
EPS = 1e-6


def rmsnorm(x, w):
    return x * (1.0 / np.sqrt(np.mean(x * x, axis=-1, keepdims=True) + EPS)) * w


def rope_tables():
    inv_freq = 1.0 / ROPE_BASE ** (np.arange(HALF) / HALF)
    ang = np.arange(S)[:, None] * inv_freq
    return np.cos(ang), np.sin(ang)


def rope(x, cos, sin):
    x1, x2 = x[..., :HALF], x[..., HALF:]
    return np.concatenate([x1 * cos - x2 * sin, x1 * sin + x2 * cos], axis=-1)


def setup_inputs():
    s, t = mx_kscale(D), mx_kscale(KVL)
    return {
        "hidden_states": bf(np.random.standard_normal((B, S, D)) * s),
        "w_kv_a": bf(np.random.standard_normal((D, KVL + ROPE)) / np.sqrt(D) / s[:, None]),
        "kv_a_ln_w": bf((1.0 + 0.1 * np.random.standard_normal(KVL)) * t),
        "w_kv_b": bf(np.random.standard_normal((KVL, H * (NOPE + VD))) / np.sqrt(KVL) / t[:, None]),
    }


def reference(hidden_states, w_kv_a, kv_a_ln_w, w_kv_b):
    fused = mxq(f64(hidden_states), 2, "e4m3") @ mxq(f64(w_kv_a), 0, "e4m3")
    kv_c, k_pe = fused[..., :KVL], fused[..., KVL:]
    kv_n = rmsnorm(kv_c, f64(kv_a_ln_w))
    kv = (mxq(kv_n, 2, "e4m3") @ mxq(f64(w_kv_b), 0, "e4m3")).reshape(B, S, H, NOPE + VD)
    k_nope, v = kv[..., :NOPE], kv[..., NOPE:]
    cos, sin = rope_tables()
    k_pe = rope(k_pe, cos[None], sin[None])
    k = np.concatenate([k_nope, np.broadcast_to(k_pe[:, :, None, :], (B, S, H, ROPE))], axis=-1)
    return k, v

@@ -1,0 +1,314 @@
+import math
+from contextlib import ExitStack
+
+import concourse.mybir as mybir
+from concourse.masks import make_identity
+
+F32 = mybir.dt.float32
+BF16 = mybir.dt.bfloat16
+I32 = mybir.dt.int32
+U32 = mybir.dt.uint32
+U8 = mybir.dt.uint8
+FP8X4 = mybir.dt.float8_e4m3fn_x4
+ALU = mybir.AluOpType
+ACT = mybir.ActivationFunctionType
+
+B, S, D, H, KVL, NOPE, ROPE, VD = 4, 1024, 512, 2, 512, 128, 128, 128
+HALF = ROPE // 2
+ROPE_BASE = 10000.0
+EPS = 1e-6
+
+P = 128
+PACK = 4
+WORD_HALVES = 2
+GROUP_TILES = 4
+GROUP_TOKENS = P * GROUP_TILES
+GROUPS = B * S // GROUP_TOKENS
+SEQ_TILES = S // P
+STEP_TILES = 2
+STEPS = GROUPS * GROUP_TILES // STEP_TILES
+STEPS_PER_GROUP = GROUP_TILES // STEP_TILES
+ROUND_TO_INTEGER = 1.5 * 2.0**23
+
+FLOPS = 2 * B * S * D * (KVL + ROPE) + 2 * B * S * KVL * H * (NOPE + VD)
+
+
+def tile_mla_pb_t_kernel(tc, hidden_states, w_kv_a, kv_a_ln_w, w_kv_b, out_0, out_1):
+    nc = tc.nc
+
+    x_groups = hidden_states.rearrange("b s d -> (b s) d").rearrange(
+        "(g p j) d -> g p (j d)", p=P, j=GROUP_TILES
+    )
+    k_groups = out_0.rearrange("b s h f -> (b s) (h f)").rearrange(
+        "(g p j) f -> g p j f", p=P, j=GROUP_TILES
+    )
+    v_groups = out_1.rearrange("b s h f -> (b s) (h f)").rearrange(
+        "(g p j) f -> g p j f", p=P, j=GROUP_TILES
+    )
+
+    with ExitStack() as ctx:
+        consts = ctx.enter_context(tc.tile_pool(name="consts", bufs=1))
+        inputs = ctx.enter_context(tc.tile_pool(name="inputs", bufs=GROUPS))
+        work = ctx.enter_context(tc.tile_pool(name="work", bufs=3))
+        results = ctx.enter_context(tc.tile_pool(name="results", bufs=3))
+        psum = ctx.enter_context(tc.psum_pool(name="psum", bufs=1))
+        ctx.enter_context(tc.manual_schedule())
+
+        def load_weight(w, columns, name):
+            rows = consts.tile([P, PACK, columns], BF16, name=name)
+            nc.sync.dma_start(
+                out=rows[:].rearrange("p (u e) c -> p u (e c)", e=2),
+                in_=w.rearrange("(u p e) c -> p u (e c)", u=WORD_HALVES, e=2),
+            )
+            return rows
+
+        x_tiles = []
+        wa_rows = load_weight(w_kv_a, KVL + ROPE, "wa_rows")
+        for g in range(GROUPS):
+            x_sb = inputs.tile([P, GROUP_TILES, D], BF16, name="x_sb")
+            nc.sync.dma_start(out=x_sb[:].rearrange("p j d -> p (j d)"), in_=x_groups[g])
+            x_tiles.append(x_sb)
+            if g == 0:
+                wb_rows = load_weight(w_kv_b, H * (NOPE + VD), "wb_rows")
+        gain = consts.tile([P, KVL], BF16)
+        nc.scalar.dma_start(out=gain[:], in_=kv_a_ln_w.partition_broadcast(P))
+
+        identity = consts.tile([P, P], F32)
+        make_identity(nc, identity[:])
+        eps = consts.tile([P, 1], F32)
+        nc.vector.memset(eps[:], EPS)
+
+        position_int = consts.tile([P, SEQ_TILES], I32)
+        nc.gpsimd.iota(
+            position_int[:],
+            pattern=[[GROUP_TOKENS, SEQ_TILES // GROUP_TILES], [1, GROUP_TILES]],
+            base=0,
+            channel_multiplier=GROUP_TILES,
+        )
+        position = consts.tile([P, SEQ_TILES], F32)
+        nc.vector.tensor_copy(out=position[:], in_=position_int[:])
+        frequency = consts.tile([P, HALF], F32)
+        nc.vector.memset(frequency[:, 0:1], 1.0)
+        done = 1
+        while done < HALF:
+            nc.vector.tensor_scalar_mul(
+                out=frequency[:, done : 2 * done],
+                in0=frequency[:, 0:done],
+                scalar1=ROPE_BASE ** (-done / HALF),
+            )
+            done *= 2
+        table_shape = [P, SEQ_TILES, HALF]
+        turns = consts.tile(table_shape, F32)
+        nc.vector.scalar_tensor_tensor(
+            out=turns[:],
+            in0=frequency[:].unsqueeze(1).to_broadcast(table_shape),
+            scalar=1.0 / (2.0 * math.pi),
+            in1=position[:].unsqueeze(2).to_broadcast(table_shape),
+            op0=ALU.mult,
+            op1=ALU.mult,
+        )
+        nearest = consts.tile(table_shape, F32)
+        nc.vector.tensor_scalar(
+            out=nearest[:],
+            in0=turns[:],
+            scalar1=ROUND_TO_INTEGER,
+            scalar2=ROUND_TO_INTEGER,
+            op0=ALU.add,
+            op1=ALU.subtract,
+        )
+        fraction = consts.tile(table_shape, F32)
+        nc.vector.tensor_tensor(out=fraction[:], in0=turns[:], in1=nearest[:], op=ALU.subtract)
+        quarter = consts.tile(table_shape, F32)
+        nc.vector.scalar_tensor_tensor(
+            out=quarter[:],
+            in0=fraction[:],
+            scalar=-1.0,
+            in1=fraction[:],
+            op0=ALU.mult,
+            op1=ALU.min,
+        )
+        nc.vector.tensor_scalar_add(out=quarter[:], in0=quarter[:], scalar1=0.25)
+        cos_table = consts.tile(table_shape, F32)
+        nc.scalar.activation(out=cos_table[:], in_=quarter[:], func=ACT.Sin, scale=2.0 * math.pi)
+        sin_table = consts.tile([P, SEQ_TILES, 2, HALF], F32)
+        nc.scalar.activation(out=sin_table[:, :, 0, :], in_=fraction[:], func=ACT.Sin, scale=-2.0 * math.pi)
+        nc.scalar.activation(out=sin_table[:, :, 1, :], in_=fraction[:], func=ACT.Sin, scale=2.0 * math.pi)
+
+        def quantise_weight(rows, column_blocks, name):
+            columns = sum(column_blocks)
+            grouped = consts.tile([P, columns, PACK], BF16, name=name + "_grouped", align_bytes=64)
+            nc.vector.tensor_copy(out=grouped[:], in_=rows[:].rearrange("p t c -> p c t"))
+            codes = consts.tile([P, columns], U32, name=name + "_codes", align_bytes=64)
+            scales = consts.tile([P, columns], U8, name=name + "_scales", align_bytes=64)
+            first = 0
+            for width in column_blocks:
+                block = slice(first, first + width)
+                nc.vector.quantize_mx(
+                    out=codes[:, block].bitcast(FP8X4),
+                    scales=scales[:, block],
+                    in_=grouped[:, block, :].rearrange("p c t -> p (c t)"),
+                )
+                first += width
+            return codes, scales
+
+        wa_codes, wa_scales = quantise_weight(wa_rows, [KVL, ROPE], "wa")
+
+        x_grouped, x_codes, x_scales = {}, {}, {}
+        kvn_rows, kvn_grouped, kvn_codes, kvn_scales = {}, {}, {}, {}
+        k_pe, k_out, v_out = {}, {}, {}
+
+        def transpose_words(rows_bf16, name):
+            words = rows_bf16.bitcast(F32)
+            flipped = psum.tile([P, STEP_TILES, WORD_HALVES, P], F32, name=name, tag="flipped", bufs=2)
+            for i in range(STEP_TILES):
+                for u in range(WORD_HALVES):
+                    nc.tensor.transpose(flipped[:, i, u, :], words[:, i, u * P : (u + 1) * P], identity[:])
+            return flipped
+
+        def new_grouped(name):
+            return work.tile([P, STEP_TILES, P, PACK], BF16, name=name, align_bytes=64)
+
+        def quantise_step(grouped, name):
+            codes = work.tile([P, STEP_TILES * P], U32, name=name + "_codes", align_bytes=64)
+            scales = work.tile([P, STEP_TILES * P], U8, name=name + "_scales", align_bytes=64)
+            nc.vector.quantize_mx(
+                out=codes[:].bitcast(FP8X4),
+                scales=scales[:],
+                in_=grouped[:].rearrange("p i t w -> p (i t w)"),
+            )
+            return codes, scales
+
+        def flip_x(step):
+            g, first_tile = step // STEPS_PER_GROUP, (step % STEPS_PER_GROUP) * STEP_TILES
+            flipped = transpose_words(x_tiles[g][:, first_tile : first_tile + STEP_TILES, :], "x_flipped")
+            x_grouped[step] = new_grouped("x_grouped")
+            nc.scalar.copy(
+                out=x_grouped[step][:].bitcast(F32), in_=flipped[:].rearrange("p i u t -> p i t u")
+            )
+
+        def flip_kvn(step):
+            flipped = transpose_words(kvn_rows[step][:], "kvn_flipped")
+            kvn_grouped[step] = new_grouped("kvn_grouped")
+            nc.vector.tensor_copy(
+                out=kvn_grouped[step][:].bitcast(F32), in_=flipped[:].rearrange("p i u t -> p i t u")
+            )
+
+        def project_down(step):
+            g, first_tile = step // STEPS_PER_GROUP, (step % STEPS_PER_GROUP) * STEP_TILES
+            k_pe[step] = psum.tile([P, STEP_TILES, ROPE], F32, name="k_pe")
+            mean_square = work.tile([P, STEP_TILES], F32, name="mean_square")
+            latents = []
+            for i in range(STEP_TILES):
+                tokens = slice(i * P, (i + 1) * P)
+                latent = psum.tile([P, KVL], F32, name="latent", bufs=3)
+                for out, columns in ((latent[:], slice(0, KVL)), (k_pe[step][:, i, :], slice(KVL, KVL + ROPE))):
+                    nc.tensor.matmul_mx(
+                        out=out,
+                        lhsT=x_codes[step][:, tokens].bitcast(FP8X4),
+                        lhsT_scale=x_scales[step][:, tokens],
+                        rhs=wa_codes[:, columns].bitcast(FP8X4),
+                        rhs_scale=wa_scales[:, columns],
+                        start=True,
+                        stop=True,
+                    )
+                squares = work.tile([P, KVL], BF16, name="squares")
+                nc.scalar.activation(
+                    out=squares[:],
+                    in_=latent[:],
+                    func=ACT.Square,
+                    scale=KVL**-0.5,
+                    accum_out=mean_square[:, i : i + 1],
+                )
+                latents.append(latent)
+            inverse_rms = work.tile([P, STEP_TILES], F32, name="inverse_rms")
+            nc.scalar.activation(
+                out=inverse_rms[:], in_=mean_square[:], func=ACT.Abs_reciprocal_sqrt, bias=eps[:], scale=1.0
+            )
+            return latents, inverse_rms
+
+        def normalise(step, latents, inverse_rms):
+            kvn_rows[step] = work.tile([P, STEP_TILES, KVL], BF16, name="kvn_rows")
+            for i in range(STEP_TILES):
+                nc.vector.scalar_tensor_tensor(
+                    out=kvn_rows[step][:, i, :],
+                    in0=latents[i][:],
+                    scalar=inverse_rms[:, i : i + 1],
+                    in1=gain[:],
+                    op0=ALU.mult,
+                    op1=ALU.mult,
+                )
+
+        def rotate(step):
+            g, first_tile = step // STEPS_PER_GROUP, (step % STEPS_PER_GROUP) * STEP_TILES
+            if first_tile == 0:
+                k_out[g] = results.tile([P, GROUP_TILES, H, NOPE + ROPE], F32, name="k_out")
+                v_out[g] = results.tile([P, GROUP_TILES, H, VD], F32, name="v_out")
+            first_entry = (g % (SEQ_TILES // GROUP_TILES)) * GROUP_TILES + first_tile
+            entries = slice(first_entry, first_entry + STEP_TILES)
+            halves = k_pe[step][:].rearrange("p j (h i) -> p j h i", h=2)
+            shape = [P, STEP_TILES, 2, HALF]
+            straight = work.tile(shape, F32, name="straight")
+            nc.vector.tensor_tensor(
+                out=straight[:],
+                in0=halves,
+                in1=cos_table[:, entries, :].unsqueeze(2).to_broadcast(shape),
+                op=ALU.mult,
+            )
+            crossed = work.tile(shape, F32, name="crossed")
+            for h in range(2):
+                nc.vector.tensor_tensor(
+                    out=crossed[:, :, h, :],
+                    in0=halves[:, :, 1 - h, :],
+                    in1=sin_table[:, entries, h, :],
+                    op=ALU.mult,
+                )
+            both_heads = [P, STEP_TILES, H, ROPE]
+            nc.gpsimd.tensor_tensor(
+                out=k_out[g][:, first_tile : first_tile + STEP_TILES, :, NOPE:],
+                in0=straight[:].rearrange("p j h i -> p j (h i)").unsqueeze(2).to_broadcast(both_heads),
+                in1=crossed[:].rearrange("p j h i -> p j (h i)").unsqueeze(2).to_broadcast(both_heads),
+                op=ALU.add,
+            )
+
+        def project_up(step):
+            g, first_tile = step // STEPS_PER_GROUP, (step % STEPS_PER_GROUP) * STEP_TILES
+            for i in range(STEP_TILES):
+                tokens = slice(i * P, (i + 1) * P)
+                kv = psum.tile([P, H, NOPE + VD], F32, name="kv", bufs=2)
+                nc.tensor.matmul_mx(
+                    out=kv[:].rearrange("p h f -> p (h f)"),
+                    lhsT=kvn_codes[step][:, tokens].bitcast(FP8X4),
+                    lhsT_scale=kvn_scales[step][:, tokens],
+                    rhs=wb_codes[:].bitcast(FP8X4),
+                    rhs_scale=wb_scales[:],
+                    start=True,
+                    stop=True,
+                )
+                nc.scalar.copy(out=k_out[g][:, first_tile + i, :, 0:NOPE], in_=kv[:, :, 0:NOPE])
+                nc.scalar.copy(out=v_out[g][:, first_tile + i, :, :], in_=kv[:, :, NOPE:])
+            tiles = slice(first_tile, first_tile + STEP_TILES)
+            nc.sync.dma_start(out=k_groups[g][:, tiles, :], in_=k_out[g][:, tiles].rearrange("p j h f -> p j (h f)"))
+            nc.sync.dma_start(out=v_groups[g][:, tiles, :], in_=v_out[g][:, tiles].rearrange("p j h f -> p j (h f)"))
+
+        def pipeline_round(rnd):
+            if rnd < STEPS:
+                flip_x(rnd)
+            if 0 <= rnd - 3 < STEPS:
+                flip_kvn(rnd - 3)
+            if rnd < STEPS:
+                x_codes[rnd], x_scales[rnd] = quantise_step(x_grouped[rnd], "x")
+            if 0 <= rnd - 1 < STEPS:
+                latents, inverse_rms = project_down(rnd - 1)
+            if 0 <= rnd - 4 < STEPS:
+                project_up(rnd - 4)
+            if 0 <= rnd - 1 < STEPS:
+                rotate(rnd - 1)
+            if 0 <= rnd - 3 < STEPS:
+                kvn_codes[rnd - 3], kvn_scales[rnd - 3] = quantise_step(kvn_grouped[rnd - 3], "kvn")
+            if 0 <= rnd - 1 < STEPS:
+                normalise(rnd - 1, latents, inverse_rms)
+
+        pipeline_round(0)
+        wb_codes, wb_scales = quantise_weight(wb_rows, [H * (NOPE + VD)], "wb")
+        for rnd in range(1, STEPS + 4):
+            pipeline_round(rnd)

@@ -70,13 +70,16 @@ def tile_mla_pb_t_kernel(tc, hidden_states, w_kv_a, kv_a_ln_w, w_kv_b, out_0, ou
             x_tiles.append(x_sb)
             if g == 0:
                 wb_rows = load_weight(w_kv_b, H * (NOPE + VD), "wb_rows")
-        gain = consts.tile([P, KVL], BF16)
-        nc.scalar.dma_start(out=gain[:], in_=kv_a_ln_w.partition_broadcast(P))
+        gain_row = consts.tile([P, KVL], BF16)
+        nc.vector.memset(gain_row[:], 0.0)
+        nc.scalar.dma_start(out=gain_row[0:1, :], in_=kv_a_ln_w.unsqueeze(0))
 
         identity = consts.tile([P, P], F32)
         make_identity(nc, identity[:])
         eps = consts.tile([P, 1], F32)
         nc.vector.memset(eps[:], EPS)
+        ones = consts.tile([P, P], BF16)
+        nc.vector.memset(ones[:], 1.0)
 
         position_int = consts.tile([P, SEQ_TILES], I32)
         nc.gpsimd.iota(
@@ -133,6 +136,8 @@ def tile_mla_pb_t_kernel(tc, hidden_states, w_kv_a, kv_a_ln_w, w_kv_b, out_0, ou
         sin_table = consts.tile([P, SEQ_TILES, 2, HALF], F32)
         nc.scalar.activation(out=sin_table[:, :, 0, :], in_=fraction[:], func=ACT.Sin, scale=-2.0 * math.pi)
         nc.scalar.activation(out=sin_table[:, :, 1, :], in_=fraction[:], func=ACT.Sin, scale=2.0 * math.pi)
+        table_warmer = consts.tile([P, 1], F32)
+        nc.scalar.activation(out=table_warmer[:], in_=eps[:], func=ACT.Abs_reciprocal_sqrt)
 
         def quantise_weight(rows, column_blocks, name):
             columns = sum(column_blocks)
@@ -155,7 +160,8 @@ def tile_mla_pb_t_kernel(tc, hidden_states, w_kv_a, kv_a_ln_w, w_kv_b, out_0, ou
 
         x_grouped, x_codes, x_scales = {}, {}, {}
         kvn_rows, kvn_grouped, kvn_codes, kvn_scales = {}, {}, {}, {}
-        k_pe, k_out, v_out = {}, {}, {}
+        k_pe, mean_square, inverse_rms, latents = {}, {}, {}, {}
+        kv_tiles, k_out, v_out = {}, {}, {}
 
         def transpose_words(rows_bf16, name):
             words = rows_bf16.bitcast(F32)
@@ -193,46 +199,57 @@ def tile_mla_pb_t_kernel(tc, hidden_states, w_kv_a, kv_a_ln_w, w_kv_b, out_0, ou
                 out=kvn_grouped[step][:].bitcast(F32), in_=flipped[:].rearrange("p i u t -> p i t u")
             )
 
-        def project_down(step):
-            g, first_tile = step // STEPS_PER_GROUP, (step % STEPS_PER_GROUP) * STEP_TILES
-            k_pe[step] = psum.tile([P, STEP_TILES, ROPE], F32, name="k_pe")
-            mean_square = work.tile([P, STEP_TILES], F32, name="mean_square")
-            latents = []
-            for i in range(STEP_TILES):
-                tokens = slice(i * P, (i + 1) * P)
-                latent = psum.tile([P, KVL], F32, name="latent", bufs=3)
-                for out, columns in ((latent[:], slice(0, KVL)), (k_pe[step][:, i, :], slice(KVL, KVL + ROPE))):
-                    nc.tensor.matmul_mx(
-                        out=out,
-                        lhsT=x_codes[step][:, tokens].bitcast(FP8X4),
-                        lhsT_scale=x_scales[step][:, tokens],
-                        rhs=wa_codes[:, columns].bitcast(FP8X4),
-                        rhs_scale=wa_scales[:, columns],
-                        start=True,
-                        stop=True,
-                    )
-                squares = work.tile([P, KVL], BF16, name="squares")
-                nc.scalar.activation(
-                    out=squares[:],
-                    in_=latent[:],
-                    func=ACT.Square,
-                    scale=KVL**-0.5,
-                    accum_out=mean_square[:, i : i + 1],
-                )
-                latents.append(latent)
-            inverse_rms = work.tile([P, STEP_TILES], F32, name="inverse_rms")
-            nc.scalar.activation(
-                out=inverse_rms[:], in_=mean_square[:], func=ACT.Abs_reciprocal_sqrt, bias=eps[:], scale=1.0
-            )
-            return latents, inverse_rms
+        def spread_gain():
+            spread = psum.tile([P, KVL], F32, name="spread", tag="latent", bufs=3)
+            nc.tensor.matmul(out=spread[:], lhsT=ones[:], rhs=gain_row[:], start=True, stop=True)
+            gain = consts.tile([P, KVL], BF16, name="gain")
+            nc.vector.tensor_copy(out=gain[:], in_=spread[:])
+            return gain
 
-        def normalise(step, latents, inverse_rms):
+        def project_down(step, i):
+            if i == 0:
+                k_pe[step] = psum.tile([P, STEP_TILES, ROPE], F32, name="k_pe")
+                mean_square[step] = work.tile([P, STEP_TILES], F32, name="mean_square")
+                inverse_rms[step] = work.tile([P, STEP_TILES], F32, name="inverse_rms")
+                latents[step] = []
+            tokens = slice(i * P, (i + 1) * P)
+            latent = psum.tile([P, KVL], F32, name="latent", tag="latent", bufs=3)
+            for out, columns in ((latent[:], slice(0, KVL)), (k_pe[step][:, i, :], slice(KVL, KVL + ROPE))):
+                nc.tensor.matmul_mx(
+                    out=out,
+                    lhsT=x_codes[step][:, tokens].bitcast(FP8X4),
+                    lhsT_scale=x_scales[step][:, tokens],
+                    rhs=wa_codes[:, columns].bitcast(FP8X4),
+                    rhs_scale=wa_scales[:, columns],
+                    start=True,
+                    stop=True,
+                )
+            squares = work.tile([P, KVL], BF16, name="squares")
+            nc.scalar.activation(
+                out=squares[:],
+                in_=latent[:],
+                func=ACT.Square,
+                scale=KVL**-0.5,
+                accum_out=mean_square[step][:, i : i + 1],
+            )
+            latents[step].append(latent)
+
+        def invert_rms(step, i):
+            nc.scalar.activation(
+                out=inverse_rms[step][:, i : i + 1],
+                in_=mean_square[step][:, i : i + 1],
+                func=ACT.Abs_reciprocal_sqrt,
+                bias=eps[:],
+                scale=1.0,
+            )
+
+        def normalise(step):
             kvn_rows[step] = work.tile([P, STEP_TILES, KVL], BF16, name="kvn_rows")
             for i in range(STEP_TILES):
                 nc.vector.scalar_tensor_tensor(
                     out=kvn_rows[step][:, i, :],
-                    in0=latents[i][:],
-                    scalar=inverse_rms[:, i : i + 1],
+                    in0=latents[step][i][:],
+                    scalar=inverse_rms[step][:, i : i + 1],
                     in1=gain[:],
                     op0=ALU.mult,
                     op1=ALU.mult,
@@ -270,45 +287,63 @@ def tile_mla_pb_t_kernel(tc, hidden_states, w_kv_a, kv_a_ln_w, w_kv_b, out_0, ou
                 op=ALU.add,
             )
 
-        def project_up(step):
+        def project_up(step, i):
+            tokens = slice(i * P, (i + 1) * P)
+            kv = psum.tile([P, H, NOPE + VD], F32, name="kv", bufs=2)
+            nc.tensor.matmul_mx(
+                out=kv[:].rearrange("p h f -> p (h f)"),
+                lhsT=kvn_codes[step][:, tokens].bitcast(FP8X4),
+                lhsT_scale=kvn_scales[step][:, tokens],
+                rhs=wb_codes[:].bitcast(FP8X4),
+                rhs_scale=wb_scales[:],
+                start=True,
+                stop=True,
+            )
+            kv_tiles[step, i] = kv
+
+        def copy_k_nope(step, i):
+            g, j = step // STEPS_PER_GROUP, (step % STEPS_PER_GROUP) * STEP_TILES + i
+            nc.scalar.copy(out=k_out[g][:, j, :, 0:NOPE], in_=kv_tiles[step, i][:, :, 0:NOPE])
+
+        def copy_v(step, i):
+            g, j = step // STEPS_PER_GROUP, (step % STEPS_PER_GROUP) * STEP_TILES + i
+            nc.scalar.copy(out=v_out[g][:, j, :, :], in_=kv_tiles[step, i][:, :, NOPE:])
+
+        def store(step):
             g, first_tile = step // STEPS_PER_GROUP, (step % STEPS_PER_GROUP) * STEP_TILES
-            for i in range(STEP_TILES):
-                tokens = slice(i * P, (i + 1) * P)
-                kv = psum.tile([P, H, NOPE + VD], F32, name="kv", bufs=2)
-                nc.tensor.matmul_mx(
-                    out=kv[:].rearrange("p h f -> p (h f)"),
-                    lhsT=kvn_codes[step][:, tokens].bitcast(FP8X4),
-                    lhsT_scale=kvn_scales[step][:, tokens],
-                    rhs=wb_codes[:].bitcast(FP8X4),
-                    rhs_scale=wb_scales[:],
-                    start=True,
-                    stop=True,
-                )
-                nc.scalar.copy(out=k_out[g][:, first_tile + i, :, 0:NOPE], in_=kv[:, :, 0:NOPE])
-                nc.scalar.copy(out=v_out[g][:, first_tile + i, :, :], in_=kv[:, :, NOPE:])
             tiles = slice(first_tile, first_tile + STEP_TILES)
             nc.sync.dma_start(out=k_groups[g][:, tiles, :], in_=k_out[g][:, tiles].rearrange("p j h f -> p j (h f)"))
             nc.sync.dma_start(out=v_groups[g][:, tiles, :], in_=v_out[g][:, tiles].rearrange("p j h f -> p j (h f)"))
 
         def pipeline_round(rnd):
-            if rnd < STEPS:
-                flip_x(rnd)
-            if 0 <= rnd - 3 < STEPS:
-                flip_kvn(rnd - 3)
-            if rnd < STEPS:
-                x_codes[rnd], x_scales[rnd] = quantise_step(x_grouped[rnd], "x")
-            if 0 <= rnd - 1 < STEPS:
-                latents, inverse_rms = project_down(rnd - 1)
-            if 0 <= rnd - 4 < STEPS:
-                project_up(rnd - 4)
-            if 0 <= rnd - 1 < STEPS:
-                rotate(rnd - 1)
-            if 0 <= rnd - 3 < STEPS:
-                kvn_codes[rnd - 3], kvn_scales[rnd - 3] = quantise_step(kvn_grouped[rnd - 3], "kvn")
-            if 0 <= rnd - 1 < STEPS:
-                normalise(rnd - 1, latents, inverse_rms)
+            entering, down, flipping, up = rnd, rnd - 1, rnd - 3, rnd - 4
+            if 0 <= entering < STEPS:
+                flip_x(entering)
+            if 0 <= flipping < STEPS:
+                flip_kvn(flipping)
+            if 0 <= entering < STEPS:
+                x_codes[entering], x_scales[entering] = quantise_step(x_grouped[entering], "x")
+            for i in range(STEP_TILES):
+                if 0 <= down < STEPS:
+                    project_down(down, i)
+                if 0 <= up < STEPS:
+                    project_up(up, i)
+                    copy_k_nope(up, i)
+                if 0 <= down < STEPS:
+                    invert_rms(down, i)
+                if 0 <= up < STEPS:
+                    copy_v(up, i)
+            if 0 <= up < STEPS:
+                store(up)
+            if 0 <= down < STEPS:
+                rotate(down)
+            if 0 <= flipping < STEPS:
+                kvn_codes[flipping], kvn_scales[flipping] = quantise_step(kvn_grouped[flipping], "kvn")
+            if 0 <= down < STEPS:
+                normalise(down)
 
         pipeline_round(0)
+        gain = spread_gain()
         wb_codes, wb_scales = quantise_weight(wb_rows, [H * (NOPE + VD)], "wb")
         for rnd in range(1, STEPS + 4):
             pipeline_round(rnd)

@@ -64,22 +64,20 @@ def tile_mla_pb_t_kernel(tc, hidden_states, w_kv_a, kv_a_ln_w, w_kv_b, out_0, ou
 
         x_tiles = []
         wa_rows = load_weight(w_kv_a, KVL + ROPE, "wa_rows")
+        gain_row = consts.tile([P, KVL], BF16)
+        nc.gpsimd.memset(gain_row[:], 0.0)
+        nc.sync.dma_start(out=gain_row[0:1, :], in_=kv_a_ln_w.unsqueeze(0))
         for g in range(GROUPS):
             x_sb = inputs.tile([P, GROUP_TILES, D], BF16, name="x_sb")
             nc.sync.dma_start(out=x_sb[:].rearrange("p j d -> p (j d)"), in_=x_groups[g])
             x_tiles.append(x_sb)
             if g == 0:
                 wb_rows = load_weight(w_kv_b, H * (NOPE + VD), "wb_rows")
-        gain_row = consts.tile([P, KVL], BF16)
-        nc.vector.memset(gain_row[:], 0.0)
-        nc.scalar.dma_start(out=gain_row[0:1, :], in_=kv_a_ln_w.unsqueeze(0))
 
-        identity = consts.tile([P, P], F32)
-        make_identity(nc, identity[:])
         eps = consts.tile([P, 1], F32)
-        nc.vector.memset(eps[:], EPS)
+        nc.gpsimd.memset(eps[:], EPS)
         ones = consts.tile([P, P], BF16)
-        nc.vector.memset(ones[:], 1.0)
+        nc.gpsimd.memset(ones[:], 1.0)
 
         position_int = consts.tile([P, SEQ_TILES], I32)
         nc.gpsimd.iota(
@@ -88,8 +86,8 @@ def tile_mla_pb_t_kernel(tc, hidden_states, w_kv_a, kv_a_ln_w, w_kv_b, out_0, ou
             base=0,
             channel_multiplier=GROUP_TILES,
         )
-        position = consts.tile([P, SEQ_TILES], F32)
-        nc.vector.tensor_copy(out=position[:], in_=position_int[:])
+        identity = consts.tile([P, P], F32)
+        make_identity(nc, identity[:])
         frequency = consts.tile([P, HALF], F32)
         nc.vector.memset(frequency[:, 0:1], 1.0)
         done = 1
@@ -100,6 +98,8 @@ def tile_mla_pb_t_kernel(tc, hidden_states, w_kv_a, kv_a_ln_w, w_kv_b, out_0, ou
                 scalar1=ROPE_BASE ** (-done / HALF),
             )
             done *= 2
+        position = consts.tile([P, SEQ_TILES], F32)
+        nc.vector.tensor_copy(out=position[:], in_=position_int[:])
         table_shape = [P, SEQ_TILES, HALF]
         turns = consts.tile(table_shape, F32)
         nc.vector.scalar_tensor_tensor(
@@ -121,6 +121,9 @@ def tile_mla_pb_t_kernel(tc, hidden_states, w_kv_a, kv_a_ln_w, w_kv_b, out_0, ou
         )
         fraction = consts.tile(table_shape, F32)
         nc.vector.tensor_tensor(out=fraction[:], in0=turns[:], in1=nearest[:], op=ALU.subtract)
+        sin_table = consts.tile([P, SEQ_TILES, 2, HALF], F32)
+        nc.scalar.activation(out=sin_table[:, :, 0, :], in_=fraction[:], func=ACT.Sin, scale=-2.0 * math.pi)
+        nc.scalar.activation(out=sin_table[:, :, 1, :], in_=fraction[:], func=ACT.Sin, scale=2.0 * math.pi)
         quarter = consts.tile(table_shape, F32)
         nc.vector.scalar_tensor_tensor(
             out=quarter[:],
@@ -133,11 +136,6 @@ def tile_mla_pb_t_kernel(tc, hidden_states, w_kv_a, kv_a_ln_w, w_kv_b, out_0, ou
         nc.vector.tensor_scalar_add(out=quarter[:], in0=quarter[:], scalar1=0.25)
         cos_table = consts.tile(table_shape, F32)
         nc.scalar.activation(out=cos_table[:], in_=quarter[:], func=ACT.Sin, scale=2.0 * math.pi)
-        sin_table = consts.tile([P, SEQ_TILES, 2, HALF], F32)
-        nc.scalar.activation(out=sin_table[:, :, 0, :], in_=fraction[:], func=ACT.Sin, scale=-2.0 * math.pi)
-        nc.scalar.activation(out=sin_table[:, :, 1, :], in_=fraction[:], func=ACT.Sin, scale=2.0 * math.pi)
-        table_warmer = consts.tile([P, 1], F32)
-        nc.scalar.activation(out=table_warmer[:], in_=eps[:], func=ACT.Abs_reciprocal_sqrt)
 
         def quantise_weight(rows, column_blocks, name):
             columns = sum(column_blocks)
@@ -343,7 +341,11 @@ def tile_mla_pb_t_kernel(tc, hidden_states, w_kv_a, kv_a_ln_w, w_kv_b, out_0, ou
                 normalise(down)
 
         pipeline_round(0)
+        table_warmer = consts.tile([P, 1], F32)
+        nc.scalar.activation(out=table_warmer[:], in_=eps[:], func=ACT.Abs_reciprocal_sqrt)
         gain = spread_gain()
+        pipeline_round(1)
+        pipeline_round(2)
         wb_codes, wb_scales = quantise_weight(wb_rows, [H * (NOPE + VD)], "wb")
-        for rnd in range(1, STEPS + 4):
+        for rnd in range(3, STEPS + 4):
             pipeline_round(rnd)

@@ -121,9 +121,9 @@ def tile_mla_pb_t_kernel(tc, hidden_states, w_kv_a, kv_a_ln_w, w_kv_b, out_0, ou
         )
         fraction = consts.tile(table_shape, F32)
         nc.vector.tensor_tensor(out=fraction[:], in0=turns[:], in1=nearest[:], op=ALU.subtract)
-        sin_table = consts.tile([P, SEQ_TILES, 2, HALF], F32)
-        nc.scalar.activation(out=sin_table[:, :, 0, :], in_=fraction[:], func=ACT.Sin, scale=-2.0 * math.pi)
-        nc.scalar.activation(out=sin_table[:, :, 1, :], in_=fraction[:], func=ACT.Sin, scale=2.0 * math.pi)
+        factors = consts.tile([P, SEQ_TILES, 4, HALF], F32)
+        nc.scalar.activation(out=factors[:, :, 2, :], in_=fraction[:], func=ACT.Sin, scale=2.0 * math.pi)
+        nc.scalar.activation(out=factors[:, :, 3, :], in_=fraction[:], func=ACT.Sin, scale=-2.0 * math.pi)
         quarter = consts.tile(table_shape, F32)
         nc.vector.scalar_tensor_tensor(
             out=quarter[:],
@@ -134,8 +134,12 @@ def tile_mla_pb_t_kernel(tc, hidden_states, w_kv_a, kv_a_ln_w, w_kv_b, out_0, ou
             op1=ALU.min,
         )
         nc.vector.tensor_scalar_add(out=quarter[:], in0=quarter[:], scalar1=0.25)
-        cos_table = consts.tile(table_shape, F32)
-        nc.scalar.activation(out=cos_table[:], in_=quarter[:], func=ACT.Sin, scale=2.0 * math.pi)
+        nc.scalar.activation(
+            out=factors[:, :, 0:2, :],
+            in_=quarter[:].unsqueeze(2).to_broadcast([P, SEQ_TILES, 2, HALF]),
+            func=ACT.Sin,
+            scale=2.0 * math.pi,
+        )
 
         def quantise_weight(rows, column_blocks, name):
             columns = sum(column_blocks)
@@ -260,30 +264,23 @@ def tile_mla_pb_t_kernel(tc, hidden_states, w_kv_a, kv_a_ln_w, w_kv_b, out_0, ou
                 v_out[g] = results.tile([P, GROUP_TILES, H, VD], F32, name="v_out")
             first_entry = (g % (SEQ_TILES // GROUP_TILES)) * GROUP_TILES + first_tile
             entries = slice(first_entry, first_entry + STEP_TILES)
-            halves = k_pe[step][:].rearrange("p j (h i) -> p j h i", h=2)
-            shape = [P, STEP_TILES, 2, HALF]
-            straight = work.tile(shape, F32, name="straight")
+            shape = [P, STEP_TILES, 2, ROPE]
+            products = work.tile(shape, F32, name="products")
             nc.vector.tensor_tensor(
-                out=straight[:],
-                in0=halves,
-                in1=cos_table[:, entries, :].unsqueeze(2).to_broadcast(shape),
+                out=products[:],
+                in0=k_pe[step][:].unsqueeze(2).to_broadcast(shape),
+                in1=factors[:, entries].rearrange("p j (s h) i -> p j s (h i)", s=2),
                 op=ALU.mult,
             )
-            crossed = work.tile(shape, F32, name="crossed")
+            both_heads = [P, STEP_TILES, H, HALF]
             for h in range(2):
-                nc.vector.tensor_tensor(
-                    out=crossed[:, :, h, :],
-                    in0=halves[:, :, 1 - h, :],
-                    in1=sin_table[:, entries, h, :],
-                    op=ALU.mult,
+                here, there = slice(h * HALF, (h + 1) * HALF), slice((1 - h) * HALF, (2 - h) * HALF)
+                nc.gpsimd.tensor_tensor(
+                    out=k_out[g][:, first_tile : first_tile + STEP_TILES, :, NOPE + h * HALF : NOPE + (h + 1) * HALF],
+                    in0=products[:, :, 0:1, here].to_broadcast(both_heads),
+                    in1=products[:, :, 1:2, there].to_broadcast(both_heads),
+                    op=ALU.add,
                 )
-            both_heads = [P, STEP_TILES, H, ROPE]
-            nc.gpsimd.tensor_tensor(
-                out=k_out[g][:, first_tile : first_tile + STEP_TILES, :, NOPE:],
-                in0=straight[:].rearrange("p j h i -> p j (h i)").unsqueeze(2).to_broadcast(both_heads),
-                in1=crossed[:].rearrange("p j h i -> p j (h i)").unsqueeze(2).to_broadcast(both_heads),
-                op=ALU.add,
-            )
 
         def project_up(step, i):
             tokens = slice(i * P, (i + 1) * P)
@@ -299,19 +296,15 @@ def tile_mla_pb_t_kernel(tc, hidden_states, w_kv_a, kv_a_ln_w, w_kv_b, out_0, ou
             )
             kv_tiles[step, i] = kv
 
-        def copy_k_nope(step, i):
+        def store_k(step, i):
             g, j = step // STEPS_PER_GROUP, (step % STEPS_PER_GROUP) * STEP_TILES + i
             nc.scalar.copy(out=k_out[g][:, j, :, 0:NOPE], in_=kv_tiles[step, i][:, :, 0:NOPE])
+            nc.sync.dma_start(out=k_groups[g][:, j, :], in_=k_out[g][:, j].rearrange("p h f -> p (h f)"))
 
-        def copy_v(step, i):
+        def store_v(step, i):
             g, j = step // STEPS_PER_GROUP, (step % STEPS_PER_GROUP) * STEP_TILES + i
             nc.scalar.copy(out=v_out[g][:, j, :, :], in_=kv_tiles[step, i][:, :, NOPE:])
-
-        def store(step):
-            g, first_tile = step // STEPS_PER_GROUP, (step % STEPS_PER_GROUP) * STEP_TILES
-            tiles = slice(first_tile, first_tile + STEP_TILES)
-            nc.sync.dma_start(out=k_groups[g][:, tiles, :], in_=k_out[g][:, tiles].rearrange("p j h f -> p j (h f)"))
-            nc.sync.dma_start(out=v_groups[g][:, tiles, :], in_=v_out[g][:, tiles].rearrange("p j h f -> p j (h f)"))
+            nc.sync.dma_start(out=v_groups[g][:, j, :], in_=v_out[g][:, j].rearrange("p h f -> p (h f)"))
 
         def pipeline_round(rnd):
             entering, down, flipping, up = rnd, rnd - 1, rnd - 3, rnd - 4
@@ -326,13 +319,11 @@ def tile_mla_pb_t_kernel(tc, hidden_states, w_kv_a, kv_a_ln_w, w_kv_b, out_0, ou
                     project_down(down, i)
                 if 0 <= up < STEPS:
                     project_up(up, i)
-                    copy_k_nope(up, i)
+                    store_k(up, i)
                 if 0 <= down < STEPS:
                     invert_rms(down, i)
                 if 0 <= up < STEPS:
-                    copy_v(up, i)
-            if 0 <= up < STEPS:
-                store(up)
+                    store_v(up, i)
             if 0 <= down < STEPS:
                 rotate(down)
             if 0 <= flipping < STEPS:

@@ -79,12 +79,13 @@ def tile_mla_pb_t_kernel(tc, hidden_states, w_kv_a, kv_a_ln_w, w_kv_b, out_0, ou
         ones = consts.tile([P, P], BF16)
         nc.gpsimd.memset(ones[:], 1.0)
 
-        position_int = consts.tile([P, SEQ_TILES], I32)
+        position = consts.tile([P, SEQ_TILES], F32)
         nc.gpsimd.iota(
-            position_int[:],
+            position[:],
             pattern=[[GROUP_TOKENS, SEQ_TILES // GROUP_TILES], [1, GROUP_TILES]],
             base=0,
             channel_multiplier=GROUP_TILES,
+            allow_small_or_imprecise_dtypes=True,
         )
         identity = consts.tile([P, P], F32)
         make_identity(nc, identity[:])
@@ -98,67 +99,82 @@ def tile_mla_pb_t_kernel(tc, hidden_states, w_kv_a, kv_a_ln_w, w_kv_b, out_0, ou
                 scalar1=ROPE_BASE ** (-done / HALF),
             )
             done *= 2
-        position = consts.tile([P, SEQ_TILES], F32)
-        nc.vector.tensor_copy(out=position[:], in_=position_int[:])
-        table_shape = [P, SEQ_TILES, HALF]
-        turns = consts.tile(table_shape, F32)
-        nc.vector.scalar_tensor_tensor(
-            out=turns[:],
-            in0=frequency[:].unsqueeze(1).to_broadcast(table_shape),
-            scalar=1.0 / (2.0 * math.pi),
-            in1=position[:].unsqueeze(2).to_broadcast(table_shape),
-            op0=ALU.mult,
-            op1=ALU.mult,
-        )
-        nearest = consts.tile(table_shape, F32)
-        nc.vector.tensor_scalar(
-            out=nearest[:],
-            in0=turns[:],
-            scalar1=ROUND_TO_INTEGER,
-            scalar2=ROUND_TO_INTEGER,
-            op0=ALU.add,
-            op1=ALU.subtract,
-        )
-        fraction = consts.tile(table_shape, F32)
-        nc.vector.tensor_tensor(out=fraction[:], in0=turns[:], in1=nearest[:], op=ALU.subtract)
-        factors = consts.tile([P, SEQ_TILES, 4, HALF], F32)
-        nc.scalar.activation(out=factors[:, :, 2, :], in_=fraction[:], func=ACT.Sin, scale=2.0 * math.pi)
-        nc.scalar.activation(out=factors[:, :, 3, :], in_=fraction[:], func=ACT.Sin, scale=-2.0 * math.pi)
-        quarter = consts.tile(table_shape, F32)
-        nc.vector.scalar_tensor_tensor(
-            out=quarter[:],
-            in0=fraction[:],
-            scalar=-1.0,
-            in1=fraction[:],
-            op0=ALU.mult,
-            op1=ALU.min,
-        )
-        nc.vector.tensor_scalar_add(out=quarter[:], in0=quarter[:], scalar1=0.25)
-        nc.scalar.activation(
-            out=factors[:, :, 0:2, :],
-            in_=quarter[:].unsqueeze(2).to_broadcast([P, SEQ_TILES, 2, HALF]),
-            func=ACT.Sin,
-            scale=2.0 * math.pi,
-        )
+        half_shape = [P, GROUP_TILES, HALF]
+        halves = range(SEQ_TILES // GROUP_TILES)
+        turns = [consts.tile(half_shape, F32, name="turns%d" % h) for h in halves]
+        nearest = [consts.tile(half_shape, F32, name="nearest%d" % h) for h in halves]
+        fraction = [consts.tile(half_shape, F32, name="fraction%d" % h) for h in halves]
+        quarter = [consts.tile(half_shape, F32, name="quarter%d" % h) for h in halves]
+        for h in halves:
+            nc.vector.scalar_tensor_tensor(
+                out=turns[h][:],
+                in0=frequency[:].unsqueeze(1).to_broadcast(half_shape),
+                scalar=1.0 / (2.0 * math.pi),
+                in1=position[:, h * GROUP_TILES : (h + 1) * GROUP_TILES].unsqueeze(2).to_broadcast(half_shape),
+                op0=ALU.mult,
+                op1=ALU.mult,
+            )
+        for h in halves:
+            nc.vector.tensor_scalar(
+                out=nearest[h][:],
+                in0=turns[h][:],
+                scalar1=ROUND_TO_INTEGER,
+                scalar2=ROUND_TO_INTEGER,
+                op0=ALU.add,
+                op1=ALU.subtract,
+            )
+        for h in halves:
+            nc.vector.tensor_tensor(out=fraction[h][:], in0=turns[h][:], in1=nearest[h][:], op=ALU.subtract)
+        for h in halves:
+            nc.vector.scalar_tensor_tensor(
+                out=quarter[h][:],
+                in0=fraction[h][:],
+                scalar=-1.0,
+                in1=fraction[h][:],
+                op0=ALU.mult,
+                op1=ALU.min,
+            )
+        for h in halves:
+            nc.vector.tensor_scalar_add(out=quarter[h][:], in0=quarter[h][:], scalar1=0.25)
+        factors = consts.tile([P, SEQ_TILES, 2, HALF], F32)
+        for h in halves:
+            entries = slice(h * GROUP_TILES, (h + 1) * GROUP_TILES)
+            nc.scalar.activation(
+                out=factors[:, entries, 1, :], in_=fraction[h][:], func=ACT.Sin, scale=2.0 * math.pi
+            )
+        for h in halves:
+            entries = slice(h * GROUP_TILES, (h + 1) * GROUP_TILES)
+            nc.scalar.activation(
+                out=factors[:, entries, 0, :],
+                in_=quarter[h][:],
+                func=ACT.Sin,
+                scale=2.0 * math.pi,
+            )
 
-        def quantise_weight(rows, column_blocks, name):
-            columns = sum(column_blocks)
-            grouped = consts.tile([P, columns, PACK], BF16, name=name + "_grouped", align_bytes=64)
-            nc.vector.tensor_copy(out=grouped[:], in_=rows[:].rearrange("p t c -> p c t"))
-            codes = consts.tile([P, columns], U32, name=name + "_codes", align_bytes=64)
-            scales = consts.tile([P, columns], U8, name=name + "_scales", align_bytes=64)
-            first = 0
-            for width in column_blocks:
-                block = slice(first, first + width)
-                nc.vector.quantize_mx(
-                    out=codes[:, block].bitcast(FP8X4),
-                    scales=scales[:, block],
-                    in_=grouped[:, block, :].rearrange("p c t -> p (c t)"),
-                )
-                first += width
-            return codes, scales
+        def new_weight(columns, name):
+            return (
+                consts.tile([P, columns, PACK], BF16, name=name + "_grouped", align_bytes=64),
+                consts.tile([P, columns], U32, name=name + "_codes", align_bytes=64),
+                consts.tile([P, columns], U8, name=name + "_scales", align_bytes=64),
+            )
 
-        wa_codes, wa_scales = quantise_weight(wa_rows, [KVL, ROPE], "wa")
+        def regroup_weight(rows, grouped, block):
+            nc.vector.tensor_copy(out=grouped[:, block, :], in_=rows[:, :, block].rearrange("p t c -> p c t"))
+
+        def quantise_weight(grouped, codes, scales, block):
+            nc.vector.quantize_mx(
+                out=codes[:, block].bitcast(FP8X4),
+                scales=scales[:, block],
+                in_=grouped[:, block, :].rearrange("p c t -> p (c t)"),
+            )
+
+        wa_grouped, wa_codes, wa_scales = new_weight(KVL + ROPE, "wa")
+        wb_grouped, wb_codes, wb_scales = new_weight(H * (NOPE + VD), "wb")
+        latent_halves = [slice(0, KVL // 2), slice(KVL // 2, KVL)]
+        for block in latent_halves:
+            regroup_weight(wa_rows, wa_grouped, block)
+        for block in latent_halves:
+            quantise_weight(wa_grouped, wa_codes, wa_scales, block)
 
         x_grouped, x_codes, x_scales = {}, {}, {}
         kvn_rows, kvn_grouped, kvn_codes, kvn_scales = {}, {}, {}, {}
@@ -264,12 +280,12 @@ def tile_mla_pb_t_kernel(tc, hidden_states, w_kv_a, kv_a_ln_w, w_kv_b, out_0, ou
                 v_out[g] = results.tile([P, GROUP_TILES, H, VD], F32, name="v_out")
             first_entry = (g % (SEQ_TILES // GROUP_TILES)) * GROUP_TILES + first_tile
             entries = slice(first_entry, first_entry + STEP_TILES)
-            shape = [P, STEP_TILES, 2, ROPE]
-            products = work.tile(shape, F32, name="products")
+            shape = [P, STEP_TILES, 2, 2, HALF]
+            products = work.tile([P, STEP_TILES, 2, ROPE], F32, name="products")
             nc.vector.tensor_tensor(
-                out=products[:],
-                in0=k_pe[step][:].unsqueeze(2).to_broadcast(shape),
-                in1=factors[:, entries].rearrange("p j (s h) i -> p j s (h i)", s=2),
+                out=products[:].rearrange("p j s (h i) -> p j s h i", h=2),
+                in0=k_pe[step][:].rearrange("p j (h i) -> p j h i", h=2).unsqueeze(2).to_broadcast(shape),
+                in1=factors[:, entries].unsqueeze(3).to_broadcast(shape),
                 op=ALU.mult,
             )
             both_heads = [P, STEP_TILES, H, HALF]
@@ -279,7 +295,7 @@ def tile_mla_pb_t_kernel(tc, hidden_states, w_kv_a, kv_a_ln_w, w_kv_b, out_0, ou
                     out=k_out[g][:, first_tile : first_tile + STEP_TILES, :, NOPE + h * HALF : NOPE + (h + 1) * HALF],
                     in0=products[:, :, 0:1, here].to_broadcast(both_heads),
                     in1=products[:, :, 1:2, there].to_broadcast(both_heads),
-                    op=ALU.add,
+                    op=ALU.subtract if h == 0 else ALU.add,
                 )
 
         def project_up(step, i):
@@ -332,11 +348,14 @@ def tile_mla_pb_t_kernel(tc, hidden_states, w_kv_a, kv_a_ln_w, w_kv_b, out_0, ou
                 normalise(down)
 
         pipeline_round(0)
+        regroup_weight(wa_rows, wa_grouped, slice(KVL, KVL + ROPE))
         table_warmer = consts.tile([P, 1], F32)
         nc.scalar.activation(out=table_warmer[:], in_=eps[:], func=ACT.Abs_reciprocal_sqrt)
         gain = spread_gain()
+        quantise_weight(wa_grouped, wa_codes, wa_scales, slice(KVL, KVL + ROPE))
         pipeline_round(1)
         pipeline_round(2)
-        wb_codes, wb_scales = quantise_weight(wb_rows, [H * (NOPE + VD)], "wb")
+        regroup_weight(wb_rows, wb_grouped, slice(0, H * (NOPE + VD)))
+        quantise_weight(wb_grouped, wb_codes, wb_scales, slice(0, H * (NOPE + VD)))
         for rnd in range(3, STEPS + 4):
             pipeline_round(rnd)

@@ -50,7 +50,7 @@ def tile_mla_pb_t_kernel(tc, hidden_states, w_kv_a, kv_a_ln_w, w_kv_b, out_0, ou
         consts = ctx.enter_context(tc.tile_pool(name="consts", bufs=1))
         inputs = ctx.enter_context(tc.tile_pool(name="inputs", bufs=GROUPS))
         work = ctx.enter_context(tc.tile_pool(name="work", bufs=3))
-        results = ctx.enter_context(tc.tile_pool(name="results", bufs=3))
+        results = ctx.enter_context(tc.tile_pool(name="results", bufs=GROUPS // 2))
         psum = ctx.enter_context(tc.psum_pool(name="psum", bufs=1))
         ctx.enter_context(tc.manual_schedule())
 
@@ -104,7 +104,7 @@ def tile_mla_pb_t_kernel(tc, hidden_states, w_kv_a, kv_a_ln_w, w_kv_b, out_0, ou
         turns = [consts.tile(half_shape, F32, name="turns%d" % h) for h in halves]
         nearest = [consts.tile(half_shape, F32, name="nearest%d" % h) for h in halves]
         fraction = [consts.tile(half_shape, F32, name="fraction%d" % h) for h in halves]
-        quarter = [consts.tile(half_shape, F32, name="quarter%d" % h) for h in halves]
+        size = [consts.tile(half_shape, F32, name="size%d" % h) for h in halves]
         for h in halves:
             nc.vector.scalar_tensor_tensor(
                 out=turns[h][:],
@@ -125,17 +125,6 @@ def tile_mla_pb_t_kernel(tc, hidden_states, w_kv_a, kv_a_ln_w, w_kv_b, out_0, ou
             )
         for h in halves:
             nc.vector.tensor_tensor(out=fraction[h][:], in0=turns[h][:], in1=nearest[h][:], op=ALU.subtract)
-        for h in halves:
-            nc.vector.scalar_tensor_tensor(
-                out=quarter[h][:],
-                in0=fraction[h][:],
-                scalar=-1.0,
-                in1=fraction[h][:],
-                op0=ALU.mult,
-                op1=ALU.min,
-            )
-        for h in halves:
-            nc.vector.tensor_scalar_add(out=quarter[h][:], in0=quarter[h][:], scalar1=0.25)
         factors = consts.tile([P, SEQ_TILES, 2, HALF], F32)
         for h in halves:
             entries = slice(h * GROUP_TILES, (h + 1) * GROUP_TILES)
@@ -143,12 +132,15 @@ def tile_mla_pb_t_kernel(tc, hidden_states, w_kv_a, kv_a_ln_w, w_kv_b, out_0, ou
                 out=factors[:, entries, 1, :], in_=fraction[h][:], func=ACT.Sin, scale=2.0 * math.pi
             )
         for h in halves:
+            nc.scalar.activation(out=size[h][:], in_=fraction[h][:], func=ACT.Abs)
+        for h in halves:
             entries = slice(h * GROUP_TILES, (h + 1) * GROUP_TILES)
             nc.scalar.activation(
                 out=factors[:, entries, 0, :],
-                in_=quarter[h][:],
+                in_=size[h][:],
                 func=ACT.Sin,
-                scale=2.0 * math.pi,
+                scale=-2.0 * math.pi,
+                bias=0.5 * math.pi,
             )
 
         def new_weight(columns, name):
@@ -189,8 +181,8 @@ def tile_mla_pb_t_kernel(tc, hidden_states, w_kv_a, kv_a_ln_w, w_kv_b, out_0, ou
                     nc.tensor.transpose(flipped[:, i, u, :], words[:, i, u * P : (u + 1) * P], identity[:])
             return flipped
 
-        def new_grouped(name):
-            return work.tile([P, STEP_TILES, P, PACK], BF16, name=name, align_bytes=64)
+        def new_grouped(name, bufs):
+            return work.tile([P, STEP_TILES, P, PACK], BF16, name=name, align_bytes=64, bufs=bufs)
 
         def quantise_step(grouped, name):
             codes = work.tile([P, STEP_TILES * P], U32, name=name + "_codes", align_bytes=64)
@@ -205,14 +197,14 @@ def tile_mla_pb_t_kernel(tc, hidden_states, w_kv_a, kv_a_ln_w, w_kv_b, out_0, ou
         def flip_x(step):
             g, first_tile = step // STEPS_PER_GROUP, (step % STEPS_PER_GROUP) * STEP_TILES
             flipped = transpose_words(x_tiles[g][:, first_tile : first_tile + STEP_TILES, :], "x_flipped")
-            x_grouped[step] = new_grouped("x_grouped")
+            x_grouped[step] = new_grouped("x_grouped", STEPS)
             nc.scalar.copy(
                 out=x_grouped[step][:].bitcast(F32), in_=flipped[:].rearrange("p i u t -> p i t u")
             )
 
         def flip_kvn(step):
             flipped = transpose_words(kvn_rows[step][:], "kvn_flipped")
-            kvn_grouped[step] = new_grouped("kvn_grouped")
+            kvn_grouped[step] = new_grouped("kvn_grouped", 3)
             nc.vector.tensor_copy(
                 out=kvn_grouped[step][:].bitcast(F32), in_=flipped[:].rearrange("p i u t -> p i t u")
             )
@@ -228,7 +220,7 @@ def tile_mla_pb_t_kernel(tc, hidden_states, w_kv_a, kv_a_ln_w, w_kv_b, out_0, ou
             if i == 0:
                 k_pe[step] = psum.tile([P, STEP_TILES, ROPE], F32, name="k_pe")
                 mean_square[step] = work.tile([P, STEP_TILES], F32, name="mean_square")
-                inverse_rms[step] = work.tile([P, STEP_TILES], F32, name="inverse_rms")
+                inverse_rms[step] = work.tile([P, STEP_TILES], F32, name="inverse_rms", bufs=STEPS)
                 latents[step] = []
             tokens = slice(i * P, (i + 1) * P)
             latent = psum.tile([P, KVL], F32, name="latent", tag="latent", bufs=3)
@@ -276,12 +268,12 @@ def tile_mla_pb_t_kernel(tc, hidden_states, w_kv_a, kv_a_ln_w, w_kv_b, out_0, ou
         def rotate(step):
             g, first_tile = step // STEPS_PER_GROUP, (step % STEPS_PER_GROUP) * STEP_TILES
             if first_tile == 0:
-                k_out[g] = results.tile([P, GROUP_TILES, H, NOPE + ROPE], F32, name="k_out")
+                k_out[g] = results.tile([P, GROUP_TILES, H, NOPE + ROPE], F32, name="k_out", bufs=GROUPS)
                 v_out[g] = results.tile([P, GROUP_TILES, H, VD], F32, name="v_out")
             first_entry = (g % (SEQ_TILES // GROUP_TILES)) * GROUP_TILES + first_tile
             entries = slice(first_entry, first_entry + STEP_TILES)
             shape = [P, STEP_TILES, 2, 2, HALF]
-            products = work.tile([P, STEP_TILES, 2, ROPE], F32, name="products")
+            products = work.tile([P, STEP_TILES, 2, ROPE], F32, name="products", bufs=STEPS)
             nc.vector.tensor_tensor(
                 out=products[:].rearrange("p j s (h i) -> p j s h i", h=2),
                 in0=k_pe[step][:].rearrange("p j (h i) -> p j h i", h=2).unsqueeze(2).to_broadcast(shape),

@@ -28,6 +28,7 @@ SEQ_TILES = S // P
 STEP_TILES = 2
 STEPS = GROUPS * GROUP_TILES // STEP_TILES
 STEPS_PER_GROUP = GROUP_TILES // STEP_TILES
+SEED = 16
 ROUND_TO_INTEGER = 1.5 * 2.0**23
 
 FLOPS = 2 * B * S * D * (KVL + ROPE) + 2 * B * S * KVL * H * (NOPE + VD)
@@ -37,7 +38,7 @@ def tile_mla_pb_t_kernel(tc, hidden_states, w_kv_a, kv_a_ln_w, w_kv_b, out_0, ou
     nc = tc.nc
 
     x_groups = hidden_states.rearrange("b s d -> (b s) d").rearrange(
-        "(g p j) d -> g p (j d)", p=P, j=GROUP_TILES
+        "(g p j) d -> g p j d", p=P, j=GROUP_TILES
     )
     k_groups = out_0.rearrange("b s h f -> (b s) (h f)").rearrange(
         "(g p j) f -> g p j f", p=P, j=GROUP_TILES
@@ -69,7 +70,9 @@ def tile_mla_pb_t_kernel(tc, hidden_states, w_kv_a, kv_a_ln_w, w_kv_b, out_0, ou
         nc.sync.dma_start(out=gain_row[0:1, :], in_=kv_a_ln_w.unsqueeze(0))
         for g in range(GROUPS):
             x_sb = inputs.tile([P, GROUP_TILES, D], BF16, name="x_sb")
-            nc.sync.dma_start(out=x_sb[:].rearrange("p j d -> p (j d)"), in_=x_groups[g])
+            for first in range(0, GROUP_TILES, STEP_TILES if g == 0 else GROUP_TILES):
+                tiles = slice(first, first + (STEP_TILES if g == 0 else GROUP_TILES))
+                nc.sync.dma_start(out=x_sb[:, tiles, :], in_=x_groups[g][:, tiles, :])
             x_tiles.append(x_sb)
             if g == 0:
                 wb_rows = load_weight(w_kv_b, H * (NOPE + VD), "wb_rows")
@@ -89,55 +92,57 @@ def tile_mla_pb_t_kernel(tc, hidden_states, w_kv_a, kv_a_ln_w, w_kv_b, out_0, ou
         )
         identity = consts.tile([P, P], F32)
         make_identity(nc, identity[:])
-        frequency = consts.tile([P, HALF], F32)
-        nc.vector.memset(frequency[:, 0:1], 1.0)
+        seed = consts.tile([P, SEED], F32)
+        nc.vector.memset(seed[:, 0:1], 1.0)
         done = 1
-        while done < HALF:
+        while done < SEED:
             nc.vector.tensor_scalar_mul(
-                out=frequency[:, done : 2 * done],
-                in0=frequency[:, 0:done],
-                scalar1=ROPE_BASE ** (-done / HALF),
+                out=seed[:, done : 2 * done], in0=seed[:, 0:done], scalar1=ROPE_BASE ** (-done / HALF)
             )
             done *= 2
-        half_shape = [P, GROUP_TILES, HALF]
-        halves = range(SEQ_TILES // GROUP_TILES)
-        turns = [consts.tile(half_shape, F32, name="turns%d" % h) for h in halves]
-        nearest = [consts.tile(half_shape, F32, name="nearest%d" % h) for h in halves]
-        fraction = [consts.tile(half_shape, F32, name="fraction%d" % h) for h in halves]
-        size = [consts.tile(half_shape, F32, name="size%d" % h) for h in halves]
-        for h in halves:
-            nc.vector.scalar_tensor_tensor(
-                out=turns[h][:],
-                in0=frequency[:].unsqueeze(1).to_broadcast(half_shape),
-                scalar=1.0 / (2.0 * math.pi),
-                in1=position[:, h * GROUP_TILES : (h + 1) * GROUP_TILES].unsqueeze(2).to_broadcast(half_shape),
-                op0=ALU.mult,
-                op1=ALU.mult,
+        turns = consts.tile([P, SEQ_TILES, HALF], F32)
+        nc.vector.scalar_tensor_tensor(
+            out=turns[:, :, 0:SEED],
+            in0=seed[:].unsqueeze(1).to_broadcast([P, SEQ_TILES, SEED]),
+            scalar=1.0 / (2.0 * math.pi),
+            in1=position[:].unsqueeze(2).to_broadcast([P, SEQ_TILES, SEED]),
+            op0=ALU.mult,
+            op1=ALU.mult,
+        )
+        for first in range(SEED, HALF, SEED):
+            nc.vector.tensor_scalar_mul(
+                out=turns[:, :, first : first + SEED],
+                in0=turns[:, :, 0:SEED],
+                scalar1=ROPE_BASE ** (-first / HALF),
             )
-        for h in halves:
+        halves = [slice(first, first + GROUP_TILES) for first in range(0, SEQ_TILES, GROUP_TILES)]
+        nearest = consts.tile([P, SEQ_TILES, HALF], F32)
+        fraction = consts.tile([P, SEQ_TILES, HALF], F32)
+        size = consts.tile([P, SEQ_TILES, HALF], F32)
+        for entries in halves:
             nc.vector.tensor_scalar(
-                out=nearest[h][:],
-                in0=turns[h][:],
+                out=nearest[:, entries],
+                in0=turns[:, entries],
                 scalar1=ROUND_TO_INTEGER,
                 scalar2=ROUND_TO_INTEGER,
                 op0=ALU.add,
                 op1=ALU.subtract,
             )
-        for h in halves:
-            nc.vector.tensor_tensor(out=fraction[h][:], in0=turns[h][:], in1=nearest[h][:], op=ALU.subtract)
-        factors = consts.tile([P, SEQ_TILES, 2, HALF], F32)
-        for h in halves:
-            entries = slice(h * GROUP_TILES, (h + 1) * GROUP_TILES)
-            nc.scalar.activation(
-                out=factors[:, entries, 1, :], in_=fraction[h][:], func=ACT.Sin, scale=2.0 * math.pi
+        for entries in halves:
+            nc.vector.tensor_tensor(
+                out=fraction[:, entries], in0=turns[:, entries], in1=nearest[:, entries], op=ALU.subtract
             )
-        for h in halves:
-            nc.scalar.activation(out=size[h][:], in_=fraction[h][:], func=ACT.Abs)
-        for h in halves:
-            entries = slice(h * GROUP_TILES, (h + 1) * GROUP_TILES)
+        factors = consts.tile([P, SEQ_TILES, 2, HALF], F32)
+        for entries in halves:
+            nc.scalar.activation(
+                out=factors[:, entries, 1, :], in_=fraction[:, entries], func=ACT.Sin, scale=2.0 * math.pi
+            )
+        for entries in halves:
+            nc.scalar.activation(out=size[:, entries], in_=fraction[:, entries], func=ACT.Abs)
+        for entries in halves:
             nc.scalar.activation(
                 out=factors[:, entries, 0, :],
-                in_=size[h][:],
+                in_=size[:, entries],
                 func=ACT.Sin,
                 scale=-2.0 * math.pi,
                 bias=0.5 * math.pi,
@@ -168,7 +173,7 @@ def tile_mla_pb_t_kernel(tc, hidden_states, w_kv_a, kv_a_ln_w, w_kv_b, out_0, ou
         for block in latent_halves:
             quantise_weight(wa_grouped, wa_codes, wa_scales, block)
 
-        x_grouped, x_codes, x_scales = {}, {}, {}
+        x_flipped, x_grouped, x_codes, x_scales = {}, {}, {}, {}
         kvn_rows, kvn_grouped, kvn_codes, kvn_scales = {}, {}, {}, {}
         k_pe, mean_square, inverse_rms, latents = {}, {}, {}, {}
         kv_tiles, k_out, v_out = {}, {}, {}
@@ -198,9 +203,10 @@ def tile_mla_pb_t_kernel(tc, hidden_states, w_kv_a, kv_a_ln_w, w_kv_b, out_0, ou
             g, first_tile = step // STEPS_PER_GROUP, (step % STEPS_PER_GROUP) * STEP_TILES
             flipped = transpose_words(x_tiles[g][:, first_tile : first_tile + STEP_TILES, :], "x_flipped")
             x_grouped[step] = new_grouped("x_grouped", STEPS)
-            nc.scalar.copy(
-                out=x_grouped[step][:].bitcast(F32), in_=flipped[:].rearrange("p i u t -> p i t u")
-            )
+            x_flipped[step] = flipped
+
+        def copy_x(step, copy):
+            copy(out=x_grouped[step][:].bitcast(F32), in_=x_flipped[step][:].rearrange("p i u t -> p i t u"))
 
         def flip_kvn(step):
             flipped = transpose_words(kvn_rows[step][:], "kvn_flipped")
@@ -216,33 +222,40 @@ def tile_mla_pb_t_kernel(tc, hidden_states, w_kv_a, kv_a_ln_w, w_kv_b, out_0, ou
             nc.vector.tensor_copy(out=gain[:], in_=spread[:])
             return gain
 
+        def project_tile(step, i, out, columns):
+            tokens = slice(i * P, (i + 1) * P)
+            nc.tensor.matmul_mx(
+                out=out,
+                lhsT=x_codes[step][:, tokens].bitcast(FP8X4),
+                lhsT_scale=x_scales[step][:, tokens],
+                rhs=wa_codes[:, columns].bitcast(FP8X4),
+                rhs_scale=wa_scales[:, columns],
+                start=True,
+                stop=True,
+            )
+
         def project_down(step, i):
             if i == 0:
                 k_pe[step] = psum.tile([P, STEP_TILES, ROPE], F32, name="k_pe")
                 mean_square[step] = work.tile([P, STEP_TILES], F32, name="mean_square")
                 inverse_rms[step] = work.tile([P, STEP_TILES], F32, name="inverse_rms", bufs=STEPS)
                 latents[step] = []
-            tokens = slice(i * P, (i + 1) * P)
             latent = psum.tile([P, KVL], F32, name="latent", tag="latent", bufs=3)
-            for out, columns in ((latent[:], slice(0, KVL)), (k_pe[step][:, i, :], slice(KVL, KVL + ROPE))):
-                nc.tensor.matmul_mx(
-                    out=out,
-                    lhsT=x_codes[step][:, tokens].bitcast(FP8X4),
-                    lhsT_scale=x_scales[step][:, tokens],
-                    rhs=wa_codes[:, columns].bitcast(FP8X4),
-                    rhs_scale=wa_scales[:, columns],
-                    start=True,
-                    stop=True,
-                )
+            project_tile(step, i, latent[:], slice(0, KVL))
+            latents[step].append(latent)
+            if i == STEP_TILES - 1:
+                for tile in range(STEP_TILES):
+                    project_tile(step, tile, k_pe[step][:, tile, :], slice(KVL, KVL + ROPE))
+
+        def square(step, i):
             squares = work.tile([P, KVL], BF16, name="squares")
             nc.scalar.activation(
                 out=squares[:],
-                in_=latent[:],
+                in_=latents[step][i][:],
                 func=ACT.Square,
                 scale=KVL**-0.5,
                 accum_out=mean_square[step][:, i : i + 1],
             )
-            latents[step].append(latent)
 
         def invert_rms(step, i):
             nc.scalar.activation(
@@ -253,17 +266,17 @@ def tile_mla_pb_t_kernel(tc, hidden_states, w_kv_a, kv_a_ln_w, w_kv_b, out_0, ou
                 scale=1.0,
             )
 
-        def normalise(step):
-            kvn_rows[step] = work.tile([P, STEP_TILES, KVL], BF16, name="kvn_rows")
-            for i in range(STEP_TILES):
-                nc.vector.scalar_tensor_tensor(
-                    out=kvn_rows[step][:, i, :],
-                    in0=latents[step][i][:],
-                    scalar=inverse_rms[step][:, i : i + 1],
-                    in1=gain[:],
-                    op0=ALU.mult,
-                    op1=ALU.mult,
-                )
+        def normalise(step, i):
+            if i == 0:
+                kvn_rows[step] = work.tile([P, STEP_TILES, KVL], BF16, name="kvn_rows")
+            nc.vector.scalar_tensor_tensor(
+                out=kvn_rows[step][:, i, :],
+                in0=latents[step][i][:],
+                scalar=inverse_rms[step][:, i : i + 1],
+                in1=gain[:],
+                op0=ALU.mult,
+                op1=ALU.mult,
+            )
 
         def rotate(step):
             g, first_tile = step // STEPS_PER_GROUP, (step % STEPS_PER_GROUP) * STEP_TILES
@@ -289,10 +302,19 @@ def tile_mla_pb_t_kernel(tc, hidden_states, w_kv_a, kv_a_ln_w, w_kv_b, out_0, ou
                     in1=products[:, :, 1:2, there].to_broadcast(both_heads),
                     op=ALU.subtract if h == 0 else ALU.add,
                 )
+            if g >= GROUPS - 2:
+                tiles = slice(first_tile, first_tile + STEP_TILES)
+                nc.sync.dma_start(
+                    out=k_groups[g][:, tiles, :].rearrange("p j (h f) -> p (j h) f", h=H)[:, :, NOPE:],
+                    in_=k_out[g][:, tiles].rearrange("p j h f -> p (j h) f")[:, :, NOPE:],
+                )
 
         def project_up(step, i):
             tokens = slice(i * P, (i + 1) * P)
-            kv = psum.tile([P, H, NOPE + VD], F32, name="kv", bufs=2)
+            if step >= STEPS - 1:
+                kv = psum.tile([P, H, NOPE + VD], F32, name="kv_last", tag="latent", bufs=3)
+            else:
+                kv = psum.tile([P, H, NOPE + VD], F32, name="kv", bufs=2)
             nc.tensor.matmul_mx(
                 out=kv[:].rearrange("p h f -> p (h f)"),
                 lhsT=kvn_codes[step][:, tokens].bitcast(FP8X4),
@@ -307,47 +329,85 @@ def tile_mla_pb_t_kernel(tc, hidden_states, w_kv_a, kv_a_ln_w, w_kv_b, out_0, ou
         def store_k(step, i):
             g, j = step // STEPS_PER_GROUP, (step % STEPS_PER_GROUP) * STEP_TILES + i
             nc.scalar.copy(out=k_out[g][:, j, :, 0:NOPE], in_=kv_tiles[step, i][:, :, 0:NOPE])
-            nc.sync.dma_start(out=k_groups[g][:, j, :], in_=k_out[g][:, j].rearrange("p h f -> p (h f)"))
+            width = NOPE if g >= GROUPS - 2 else NOPE + ROPE
+            nc.sync.dma_start(
+                out=k_groups[g][:, j, :].rearrange("p (h f) -> p h f", h=H)[:, :, 0:width],
+                in_=k_out[g][:, j, :, 0:width],
+            )
 
         def store_v(step, i):
             g, j = step // STEPS_PER_GROUP, (step % STEPS_PER_GROUP) * STEP_TILES + i
-            nc.scalar.copy(out=v_out[g][:, j, :, :], in_=kv_tiles[step, i][:, :, NOPE:])
+            copy = nc.vector.tensor_copy if step >= STEPS - 2 else nc.scalar.copy
+            copy(out=v_out[g][:, j, :, :], in_=kv_tiles[step, i][:, :, NOPE:])
             nc.sync.dma_start(out=v_groups[g][:, j, :], in_=v_out[g][:, j].rearrange("p h f -> p (h f)"))
 
+        def quantise_x(step):
+            x_codes[step], x_scales[step] = quantise_step(x_grouped[step], "x")
+
         def pipeline_round(rnd):
-            entering, down, flipping, up = rnd, rnd - 1, rnd - 3, rnd - 4
+            entering, down, flipping, up = rnd + 2, rnd, rnd - 2, rnd - 3
+            filling = flipping < 0
             if 0 <= entering < STEPS:
                 flip_x(entering)
+                if not filling:
+                    copy_x(entering, nc.scalar.copy)
             if 0 <= flipping < STEPS:
                 flip_kvn(flipping)
-            if 0 <= entering < STEPS:
-                x_codes[entering], x_scales[entering] = quantise_step(x_grouped[entering], "x")
+            if 0 <= entering < STEPS and not filling:
+                quantise_x(entering)
             for i in range(STEP_TILES):
                 if 0 <= down < STEPS:
                     project_down(down, i)
+                    square(down, i)
+                if filling and i == 0:
+                    copy_x(entering, nc.scalar.copy)
                 if 0 <= up < STEPS:
                     project_up(up, i)
                     store_k(up, i)
                 if 0 <= down < STEPS:
                     invert_rms(down, i)
-                if 0 <= up < STEPS:
+                if 0 <= up < STEPS - 2:
                     store_v(up, i)
             if 0 <= down < STEPS:
                 rotate(down)
             if 0 <= flipping < STEPS:
                 kvn_codes[flipping], kvn_scales[flipping] = quantise_step(kvn_grouped[flipping], "kvn")
             if 0 <= down < STEPS:
-                normalise(down)
+                normalise(down, 0)
+                if filling:
+                    quantise_x(entering)
+                normalise(down, 1)
+            if STEPS - 2 <= up < STEPS:
+                for i in range(STEP_TILES):
+                    store_v(up, i)
 
-        pipeline_round(0)
-        regroup_weight(wa_rows, wa_grouped, slice(KVL, KVL + ROPE))
+        def regroup_on_gpsimd(block):
+            nc.gpsimd.tensor_scalar(
+                out=wb_grouped[:, block, :],
+                in0=wb_rows[:, :, block].rearrange("p t c -> p c t"),
+                scalar1=1.0,
+                scalar2=0.0,
+                op0=ALU.mult,
+                op1=ALU.add,
+            )
+
+        flip_x(0)
+        copy_x(0, nc.scalar.copy)
+        quantise_x(0)
         table_warmer = consts.tile([P, 1], F32)
         nc.scalar.activation(out=table_warmer[:], in_=eps[:], func=ACT.Abs_reciprocal_sqrt)
-        gain = spread_gain()
+        flip_x(1)
+        regroup_weight(wa_rows, wa_grouped, slice(KVL, KVL + ROPE))
+        copy_x(1, nc.vector.tensor_copy)
         quantise_weight(wa_grouped, wa_codes, wa_scales, slice(KVL, KVL + ROPE))
+        quantise_x(1)
+        gain = spread_gain()
+        for block in range(0, 256, 128):
+            regroup_on_gpsimd(slice(block, block + 128))
+        pipeline_round(0)
+        for block in range(256, 512, 128):
+            regroup_on_gpsimd(slice(block, block + 128))
         pipeline_round(1)
-        pipeline_round(2)
-        regroup_weight(wb_rows, wb_grouped, slice(0, H * (NOPE + VD)))
         quantise_weight(wb_grouped, wb_codes, wb_scales, slice(0, H * (NOPE + VD)))
-        for rnd in range(3, STEPS + 4):
+        for rnd in range(2, STEPS + 3):
             pipeline_round(rnd)

@@ -28,6 +28,8 @@ SEQ_TILES = S // P
 STEP_TILES = 2
 STEPS = GROUPS * GROUP_TILES // STEP_TILES
 STEPS_PER_GROUP = GROUP_TILES // STEP_TILES
+X_LEAD = 2
+KVN_LAG = 2
 SEED = 16
 ROUND_TO_INTEGER = 1.5 * 2.0**23
 
@@ -173,8 +175,8 @@ def tile_mla_pb_t_kernel(tc, hidden_states, w_kv_a, kv_a_ln_w, w_kv_b, out_0, ou
         for block in latent_halves:
             quantise_weight(wa_grouped, wa_codes, wa_scales, block)
 
-        x_flipped, x_grouped, x_codes, x_scales = {}, {}, {}, {}
-        kvn_rows, kvn_grouped, kvn_codes, kvn_scales = {}, {}, {}, {}
+        x_flipped, kvn_rows = {}, {}
+        grouped, codes, scales = {}, {}, {}
         k_pe, mean_square, inverse_rms, latents = {}, {}, {}, {}
         kv_tiles, k_out, v_out = {}, {}, {}
 
@@ -186,33 +188,45 @@ def tile_mla_pb_t_kernel(tc, hidden_states, w_kv_a, kv_a_ln_w, w_kv_b, out_0, ou
                     nc.tensor.transpose(flipped[:, i, u, :], words[:, i, u * P : (u + 1) * P], identity[:])
             return flipped
 
-        def new_grouped(name, bufs):
-            return work.tile([P, STEP_TILES, P, PACK], BF16, name=name, align_bytes=64, bufs=bufs)
+        def new_pair(rnd):
+            grouped[rnd] = work.tile([P, 2, STEP_TILES, P, PACK], BF16, name="grouped", align_bytes=64, bufs=STEPS // 2)
+            codes[rnd] = work.tile([P, 2, STEP_TILES * P], U32, name="codes", align_bytes=64, bufs=4)
+            scales[rnd] = work.tile([P, 2, STEP_TILES * P], U8, name="scales", align_bytes=64, bufs=4)
 
-        def quantise_step(grouped, name):
-            codes = work.tile([P, STEP_TILES * P], U32, name=name + "_codes", align_bytes=64)
-            scales = work.tile([P, STEP_TILES * P], U8, name=name + "_scales", align_bytes=64)
+        def quantise_pair(rnd):
+            kinds = slice(0 if rnd + X_LEAD < STEPS else 1, 2 if rnd >= KVN_LAG else 1)
             nc.vector.quantize_mx(
-                out=codes[:].bitcast(FP8X4),
-                scales=scales[:],
-                in_=grouped[:].rearrange("p i t w -> p (i t w)"),
+                out=codes[rnd][:, kinds, :].rearrange("p k c -> p (k c)").bitcast(FP8X4),
+                scales=scales[rnd][:, kinds, :].rearrange("p k c -> p (k c)"),
+                in_=grouped[rnd][:, kinds].rearrange("p k i t w -> p (k i t w)"),
             )
-            return codes, scales
+
+        def multiply(out, pair, kind, i, weight_codes, weight_scales):
+            tokens = slice(i * P, (i + 1) * P)
+            nc.tensor.matmul_mx(
+                out=out,
+                lhsT=codes[pair][:, kind, tokens].bitcast(FP8X4),
+                lhsT_scale=scales[pair][:, kind, tokens],
+                rhs=weight_codes.bitcast(FP8X4),
+                rhs_scale=weight_scales,
+                start=True,
+                stop=True,
+            )
 
         def flip_x(step):
             g, first_tile = step // STEPS_PER_GROUP, (step % STEPS_PER_GROUP) * STEP_TILES
-            flipped = transpose_words(x_tiles[g][:, first_tile : first_tile + STEP_TILES, :], "x_flipped")
-            x_grouped[step] = new_grouped("x_grouped", STEPS)
-            x_flipped[step] = flipped
+            x_flipped[step] = transpose_words(x_tiles[g][:, first_tile : first_tile + STEP_TILES, :], "x_words")
 
         def copy_x(step, copy):
-            copy(out=x_grouped[step][:].bitcast(F32), in_=x_flipped[step][:].rearrange("p i u t -> p i t u"))
+            copy(
+                out=grouped[step - X_LEAD][:, 0].bitcast(F32), in_=x_flipped[step][:].rearrange("p i u t -> p i t u")
+            )
 
         def flip_kvn(step):
             flipped = transpose_words(kvn_rows[step][:], "kvn_flipped")
-            kvn_grouped[step] = new_grouped("kvn_grouped", 3)
-            nc.vector.tensor_copy(
-                out=kvn_grouped[step][:].bitcast(F32), in_=flipped[:].rearrange("p i u t -> p i t u")
+            copy = nc.scalar.copy if step == STEPS - 2 else nc.vector.tensor_copy
+            copy(
+                out=grouped[step + KVN_LAG][:, 1].bitcast(F32), in_=flipped[:].rearrange("p i u t -> p i t u")
             )
 
         def spread_gain():
@@ -222,18 +236,6 @@ def tile_mla_pb_t_kernel(tc, hidden_states, w_kv_a, kv_a_ln_w, w_kv_b, out_0, ou
             nc.vector.tensor_copy(out=gain[:], in_=spread[:])
             return gain
 
-        def project_tile(step, i, out, columns):
-            tokens = slice(i * P, (i + 1) * P)
-            nc.tensor.matmul_mx(
-                out=out,
-                lhsT=x_codes[step][:, tokens].bitcast(FP8X4),
-                lhsT_scale=x_scales[step][:, tokens],
-                rhs=wa_codes[:, columns].bitcast(FP8X4),
-                rhs_scale=wa_scales[:, columns],
-                start=True,
-                stop=True,
-            )
-
         def project_down(step, i):
             if i == 0:
                 k_pe[step] = psum.tile([P, STEP_TILES, ROPE], F32, name="k_pe")
@@ -241,11 +243,14 @@ def tile_mla_pb_t_kernel(tc, hidden_states, w_kv_a, kv_a_ln_w, w_kv_b, out_0, ou
                 inverse_rms[step] = work.tile([P, STEP_TILES], F32, name="inverse_rms", bufs=STEPS)
                 latents[step] = []
             latent = psum.tile([P, KVL], F32, name="latent", tag="latent", bufs=3)
-            project_tile(step, i, latent[:], slice(0, KVL))
+            multiply(latent[:], step - X_LEAD, 0, i, wa_codes[:, 0:KVL], wa_scales[:, 0:KVL])
             latents[step].append(latent)
             if i == STEP_TILES - 1:
+                columns = slice(KVL, KVL + ROPE)
                 for tile in range(STEP_TILES):
-                    project_tile(step, tile, k_pe[step][:, tile, :], slice(KVL, KVL + ROPE))
+                    multiply(
+                        k_pe[step][:, tile, :], step - X_LEAD, 0, tile, wa_codes[:, columns], wa_scales[:, columns]
+                    )
 
         def square(step, i):
             squares = work.tile([P, KVL], BF16, name="squares")
@@ -310,20 +315,11 @@ def tile_mla_pb_t_kernel(tc, hidden_states, w_kv_a, kv_a_ln_w, w_kv_b, out_0, ou
                 )
 
         def project_up(step, i):
-            tokens = slice(i * P, (i + 1) * P)
             if step >= STEPS - 1:
                 kv = psum.tile([P, H, NOPE + VD], F32, name="kv_last", tag="latent", bufs=3)
             else:
                 kv = psum.tile([P, H, NOPE + VD], F32, name="kv", bufs=2)
-            nc.tensor.matmul_mx(
-                out=kv[:].rearrange("p h f -> p (h f)"),
-                lhsT=kvn_codes[step][:, tokens].bitcast(FP8X4),
-                lhsT_scale=kvn_scales[step][:, tokens],
-                rhs=wb_codes[:].bitcast(FP8X4),
-                rhs_scale=wb_scales[:],
-                start=True,
-                stop=True,
-            )
+            multiply(kv[:].rearrange("p h f -> p (h f)"), step + KVN_LAG, 1, i, wb_codes[:], wb_scales[:])
             kv_tiles[step, i] = kv
 
         def store_k(step, i):
@@ -341,20 +337,16 @@ def tile_mla_pb_t_kernel(tc, hidden_states, w_kv_a, kv_a_ln_w, w_kv_b, out_0, ou
             copy(out=v_out[g][:, j, :, :], in_=kv_tiles[step, i][:, :, NOPE:])
             nc.sync.dma_start(out=v_groups[g][:, j, :], in_=v_out[g][:, j].rearrange("p h f -> p (h f)"))
 
-        def quantise_x(step):
-            x_codes[step], x_scales[step] = quantise_step(x_grouped[step], "x")
-
         def pipeline_round(rnd):
-            entering, down, flipping, up = rnd + 2, rnd, rnd - 2, rnd - 3
+            entering, down, flipping, up = rnd + X_LEAD, rnd, rnd - KVN_LAG, rnd - KVN_LAG - 1
             filling = flipping < 0
+            new_pair(rnd)
             if 0 <= entering < STEPS:
                 flip_x(entering)
                 if not filling:
                     copy_x(entering, nc.scalar.copy)
             if 0 <= flipping < STEPS:
                 flip_kvn(flipping)
-            if 0 <= entering < STEPS and not filling:
-                quantise_x(entering)
             for i in range(STEP_TILES):
                 if 0 <= down < STEPS:
                     project_down(down, i)
@@ -371,11 +363,11 @@ def tile_mla_pb_t_kernel(tc, hidden_states, w_kv_a, kv_a_ln_w, w_kv_b, out_0, ou
             if 0 <= down < STEPS:
                 rotate(down)
             if 0 <= flipping < STEPS:
-                kvn_codes[flipping], kvn_scales[flipping] = quantise_step(kvn_grouped[flipping], "kvn")
+                quantise_pair(rnd)
             if 0 <= down < STEPS:
                 normalise(down, 0)
                 if filling:
-                    quantise_x(entering)
+                    quantise_pair(rnd)
                 normalise(down, 1)
             if STEPS - 2 <= up < STEPS:
                 for i in range(STEP_TILES):
@@ -391,23 +383,27 @@ def tile_mla_pb_t_kernel(tc, hidden_states, w_kv_a, kv_a_ln_w, w_kv_b, out_0, ou
                 op1=ALU.add,
             )
 
+        new_pair(-2)
         flip_x(0)
         copy_x(0, nc.scalar.copy)
-        quantise_x(0)
+        gain = spread_gain()
+        quantise_pair(-2)
         table_warmer = consts.tile([P, 1], F32)
         nc.scalar.activation(out=table_warmer[:], in_=eps[:], func=ACT.Abs_reciprocal_sqrt)
+        new_pair(-1)
         flip_x(1)
         regroup_weight(wa_rows, wa_grouped, slice(KVL, KVL + ROPE))
         copy_x(1, nc.vector.tensor_copy)
         quantise_weight(wa_grouped, wa_codes, wa_scales, slice(KVL, KVL + ROPE))
-        quantise_x(1)
-        gain = spread_gain()
-        for block in range(0, 256, 128):
+        quantise_pair(-1)
+        for block in range(0, 384, 128):
             regroup_on_gpsimd(slice(block, block + 128))
         pipeline_round(0)
-        for block in range(256, 512, 128):
-            regroup_on_gpsimd(slice(block, block + 128))
+        for block in range(384, 512, 128):
+            regroup_on_gpsimd(slice(block, min(block + 128, 512)))
         pipeline_round(1)
+        for block in range(512, 512, 128):
+            regroup_on_gpsimd(slice(block, block + 128))
         quantise_weight(wb_grouped, wb_codes, wb_scales, slice(0, H * (NOPE + VD)))
-        for rnd in range(2, STEPS + 3):
+        for rnd in range(2, STEPS + KVN_LAG + 1):
             pipeline_round(rnd)

@@ -65,20 +65,23 @@ def tile_mla_pb_t_kernel(tc, hidden_states, w_kv_a, kv_a_ln_w, w_kv_b, out_0, ou
             )
             return rows
 
-        x_tiles = []
+        x_tiles = [inputs.tile([P, GROUP_TILES, D], BF16, name="x_sb") for g in range(GROUPS)]
+
+        def load_x(g, first, count):
+            tiles = slice(first, first + count)
+            nc.sync.dma_start(out=x_tiles[g][:, tiles, :], in_=x_groups[g][:, tiles, :])
+
+        load_x(0, 0, STEP_TILES)
         wa_rows = load_weight(w_kv_a, KVL + ROPE, "wa_rows")
         gain_row = consts.tile([P, KVL], BF16)
         nc.gpsimd.memset(gain_row[:], 0.0)
         nc.sync.dma_start(out=gain_row[0:1, :], in_=kv_a_ln_w.unsqueeze(0))
-        for g in range(GROUPS):
-            x_sb = inputs.tile([P, GROUP_TILES, D], BF16, name="x_sb")
-            for first in range(0, GROUP_TILES, STEP_TILES if g == 0 else GROUP_TILES):
-                tiles = slice(first, first + (STEP_TILES if g == 0 else GROUP_TILES))
-                nc.sync.dma_start(out=x_sb[:, tiles, :], in_=x_groups[g][:, tiles, :])
-            x_tiles.append(x_sb)
-            if g == 0:
-                wb_rows = load_weight(w_kv_b, H * (NOPE + VD), "wb_rows")
+        load_x(0, STEP_TILES, STEP_TILES)
+        wb_rows = load_weight(w_kv_b, H * (NOPE + VD), "wb_rows")
+        for g in range(1, GROUPS):
+            load_x(g, 0, GROUP_TILES)
 
+        table_warmer = consts.tile([P, 1], F32)
         eps = consts.tile([P, 1], F32)
         nc.gpsimd.memset(eps[:], EPS)
         ones = consts.tile([P, P], BF16)
@@ -134,22 +137,6 @@ def tile_mla_pb_t_kernel(tc, hidden_states, w_kv_a, kv_a_ln_w, w_kv_b, out_0, ou
             nc.vector.tensor_tensor(
                 out=fraction[:, entries], in0=turns[:, entries], in1=nearest[:, entries], op=ALU.subtract
             )
-        factors = consts.tile([P, SEQ_TILES, 2, HALF], F32)
-        for entries in halves:
-            nc.scalar.activation(
-                out=factors[:, entries, 1, :], in_=fraction[:, entries], func=ACT.Sin, scale=2.0 * math.pi
-            )
-        for entries in halves:
-            nc.scalar.activation(out=size[:, entries], in_=fraction[:, entries], func=ACT.Abs)
-        for entries in halves:
-            nc.scalar.activation(
-                out=factors[:, entries, 0, :],
-                in_=size[:, entries],
-                func=ACT.Sin,
-                scale=-2.0 * math.pi,
-                bias=0.5 * math.pi,
-            )
-
         def new_weight(columns, name):
             return (
                 consts.tile([P, columns, PACK], BF16, name=name + "_grouped", align_bytes=64),
@@ -158,7 +145,10 @@ def tile_mla_pb_t_kernel(tc, hidden_states, w_kv_a, kv_a_ln_w, w_kv_b, out_0, ou
             )
 
         def regroup_weight(rows, grouped, block):
-            nc.vector.tensor_copy(out=grouped[:, block, :], in_=rows[:, :, block].rearrange("p t c -> p c t"))
+            nc.vector.tensor_copy(
+                out=grouped[:, block, :].rearrange("p (c i) t -> p c t i", i=PACK),
+                in_=rows[:, :, block].rearrange("p t (c i) -> p c t i", i=PACK),
+            )
 
         def quantise_weight(grouped, codes, scales, block):
             nc.vector.quantize_mx(
@@ -169,12 +159,6 @@ def tile_mla_pb_t_kernel(tc, hidden_states, w_kv_a, kv_a_ln_w, w_kv_b, out_0, ou
 
         wa_grouped, wa_codes, wa_scales = new_weight(KVL + ROPE, "wa")
         wb_grouped, wb_codes, wb_scales = new_weight(H * (NOPE + VD), "wb")
-        latent_halves = [slice(0, KVL // 2), slice(KVL // 2, KVL)]
-        for block in latent_halves:
-            regroup_weight(wa_rows, wa_grouped, block)
-        for block in latent_halves:
-            quantise_weight(wa_grouped, wa_codes, wa_scales, block)
-
         x_flipped, kvn_rows = {}, {}
         grouped, codes, scales = {}, {}, {}
         k_pe, mean_square, inverse_rms, latents = {}, {}, {}, {}
@@ -224,13 +208,13 @@ def tile_mla_pb_t_kernel(tc, hidden_states, w_kv_a, kv_a_ln_w, w_kv_b, out_0, ou
 
         def flip_kvn(step):
             flipped = transpose_words(kvn_rows[step][:], "kvn_flipped")
-            copy = nc.scalar.copy if step == STEPS - 2 else nc.vector.tensor_copy
+            copy = nc.scalar.copy if step in (0, STEPS - 2) else nc.vector.tensor_copy
             copy(
                 out=grouped[step + KVN_LAG][:, 1].bitcast(F32), in_=flipped[:].rearrange("p i u t -> p i t u")
             )
 
         def spread_gain():
-            spread = psum.tile([P, KVL], F32, name="spread", tag="latent", bufs=3)
+            spread = psum.tile([P, KVL], BF16, name="spread", tag="latent", bufs=3)
             nc.tensor.matmul(out=spread[:], lhsT=ones[:], rhs=gain_row[:], start=True, stop=True)
             gain = consts.tile([P, KVL], BF16, name="gain")
             nc.vector.tensor_copy(out=gain[:], in_=spread[:])
@@ -341,10 +325,9 @@ def tile_mla_pb_t_kernel(tc, hidden_states, w_kv_a, kv_a_ln_w, w_kv_b, out_0, ou
             entering, down, flipping, up = rnd + X_LEAD, rnd, rnd - KVN_LAG, rnd - KVN_LAG - 1
             filling = flipping < 0
             new_pair(rnd)
-            if 0 <= entering < STEPS:
+            if 0 <= entering < STEPS and not filling:
                 flip_x(entering)
-                if not filling:
-                    copy_x(entering, nc.scalar.copy)
+                copy_x(entering, nc.scalar.copy)
             if 0 <= flipping < STEPS:
                 flip_kvn(flipping)
             for i in range(STEP_TILES):
@@ -352,6 +335,7 @@ def tile_mla_pb_t_kernel(tc, hidden_states, w_kv_a, kv_a_ln_w, w_kv_b, out_0, ou
                     project_down(down, i)
                     square(down, i)
                 if filling and i == 0:
+                    flip_x(entering)
                     copy_x(entering, nc.scalar.copy)
                 if 0 <= up < STEPS:
                     project_up(up, i)
@@ -385,10 +369,31 @@ def tile_mla_pb_t_kernel(tc, hidden_states, w_kv_a, kv_a_ln_w, w_kv_b, out_0, ou
 
         new_pair(-2)
         flip_x(0)
+        nc.scalar.activation(out=table_warmer[:], in_=eps[:], func=ACT.Sin)
         copy_x(0, nc.scalar.copy)
-        gain = spread_gain()
+        factors = consts.tile([P, SEQ_TILES, 2, HALF], F32)
+        for entries in halves:
+            nc.scalar.activation(
+                out=factors[:, entries, 1, :], in_=fraction[:, entries], func=ACT.Sin, scale=2.0 * math.pi
+            )
+        for entries in halves:
+            nc.scalar.activation(out=size[:, entries], in_=fraction[:, entries], func=ACT.Abs)
+        for entries in halves:
+            nc.scalar.activation(
+                out=factors[:, entries, 0, :],
+                in_=size[:, entries],
+                func=ACT.Sin,
+                scale=-2.0 * math.pi,
+                bias=0.5 * math.pi,
+            )
+
+        latent_halves = [slice(0, KVL // 2), slice(KVL // 2, KVL)]
+        regroup_weight(wa_rows, wa_grouped, latent_halves[0])
         quantise_pair(-2)
-        table_warmer = consts.tile([P, 1], F32)
+        regroup_weight(wa_rows, wa_grouped, latent_halves[1])
+        for block in latent_halves:
+            quantise_weight(wa_grouped, wa_codes, wa_scales, block)
+        gain = spread_gain()
         nc.scalar.activation(out=table_warmer[:], in_=eps[:], func=ACT.Abs_reciprocal_sqrt)
         new_pair(-1)
         flip_x(1)
@@ -400,10 +405,8 @@ def tile_mla_pb_t_kernel(tc, hidden_states, w_kv_a, kv_a_ln_w, w_kv_b, out_0, ou
             regroup_on_gpsimd(slice(block, block + 128))
         pipeline_round(0)
         for block in range(384, 512, 128):
-            regroup_on_gpsimd(slice(block, min(block + 128, 512)))
-        pipeline_round(1)
-        for block in range(512, 512, 128):
             regroup_on_gpsimd(slice(block, block + 128))
+        pipeline_round(1)
         quantise_weight(wb_grouped, wb_codes, wb_scales, slice(0, H * (NOPE + VD)))
         for rnd in range(2, STEPS + KVN_LAG + 1):
             pipeline_round(rnd)

@@ -42,9 +42,7 @@ def tile_mla_pb_t_kernel(tc, hidden_states, w_kv_a, kv_a_ln_w, w_kv_b, out_0, ou
     x_groups = hidden_states.rearrange("b s d -> (b s) d").rearrange(
         "(g p j) d -> g p j d", p=P, j=GROUP_TILES
     )
-    k_groups = out_0.rearrange("b s h f -> (b s) (h f)").rearrange(
-        "(g p j) f -> g p j f", p=P, j=GROUP_TILES
-    )
+    k_heads = out_0.rearrange("b s h f -> (b s) h f").rearrange("(g p j) h f -> g p j h f", p=P, j=GROUP_TILES)
     v_groups = out_1.rearrange("b s h f -> (b s) (h f)").rearrange(
         "(g p j) f -> g p j f", p=P, j=GROUP_TILES
     )
@@ -53,7 +51,7 @@ def tile_mla_pb_t_kernel(tc, hidden_states, w_kv_a, kv_a_ln_w, w_kv_b, out_0, ou
         consts = ctx.enter_context(tc.tile_pool(name="consts", bufs=1))
         inputs = ctx.enter_context(tc.tile_pool(name="inputs", bufs=GROUPS))
         work = ctx.enter_context(tc.tile_pool(name="work", bufs=3))
-        results = ctx.enter_context(tc.tile_pool(name="results", bufs=GROUPS // 2))
+        results = ctx.enter_context(tc.tile_pool(name="results", bufs=GROUPS))
         psum = ctx.enter_context(tc.psum_pool(name="psum", bufs=1))
         ctx.enter_context(tc.manual_schedule())
 
@@ -162,7 +160,7 @@ def tile_mla_pb_t_kernel(tc, hidden_states, w_kv_a, kv_a_ln_w, w_kv_b, out_0, ou
         x_flipped, kvn_rows = {}, {}
         grouped, codes, scales = {}, {}, {}
         k_pe, mean_square, inverse_rms, latents = {}, {}, {}, {}
-        kv_tiles, k_out, v_out = {}, {}, {}
+        kv_tiles, kv_out, rope_out = {}, {}, {}
 
         def transpose_words(rows_bf16, name):
             words = rows_bf16.bitcast(F32)
@@ -270,8 +268,8 @@ def tile_mla_pb_t_kernel(tc, hidden_states, w_kv_a, kv_a_ln_w, w_kv_b, out_0, ou
         def rotate(step):
             g, first_tile = step // STEPS_PER_GROUP, (step % STEPS_PER_GROUP) * STEP_TILES
             if first_tile == 0:
-                k_out[g] = results.tile([P, GROUP_TILES, H, NOPE + ROPE], F32, name="k_out", bufs=GROUPS)
-                v_out[g] = results.tile([P, GROUP_TILES, H, VD], F32, name="v_out")
+                kv_out[g] = results.tile([P, GROUP_TILES, 2, H, P], F32, name="kv_out")
+                rope_out[g] = results.tile([P, GROUP_TILES, ROPE], F32, name="rope_out")
             first_entry = (g % (SEQ_TILES // GROUP_TILES)) * GROUP_TILES + first_tile
             entries = slice(first_entry, first_entry + STEP_TILES)
             shape = [P, STEP_TILES, 2, 2, HALF]
@@ -282,44 +280,35 @@ def tile_mla_pb_t_kernel(tc, hidden_states, w_kv_a, kv_a_ln_w, w_kv_b, out_0, ou
                 in1=factors[:, entries].unsqueeze(3).to_broadcast(shape),
                 op=ALU.mult,
             )
-            both_heads = [P, STEP_TILES, H, HALF]
-            for h in range(2):
-                here, there = slice(h * HALF, (h + 1) * HALF), slice((1 - h) * HALF, (2 - h) * HALF)
+            tiles = slice(first_tile, first_tile + STEP_TILES)
+            for half in range(2):
+                here, there = slice(half * HALF, (half + 1) * HALF), slice((1 - half) * HALF, (2 - half) * HALF)
                 nc.gpsimd.tensor_tensor(
-                    out=k_out[g][:, first_tile : first_tile + STEP_TILES, :, NOPE + h * HALF : NOPE + (h + 1) * HALF],
-                    in0=products[:, :, 0:1, here].to_broadcast(both_heads),
-                    in1=products[:, :, 1:2, there].to_broadcast(both_heads),
-                    op=ALU.subtract if h == 0 else ALU.add,
+                    out=rope_out[g][:, tiles, here],
+                    in0=products[:, :, 0, here],
+                    in1=products[:, :, 1, there],
+                    op=ALU.subtract if half == 0 else ALU.add,
                 )
-            if g >= GROUPS - 2:
-                tiles = slice(first_tile, first_tile + STEP_TILES)
+            for h in range(H):
                 nc.sync.dma_start(
-                    out=k_groups[g][:, tiles, :].rearrange("p j (h f) -> p (j h) f", h=H)[:, :, NOPE:],
-                    in_=k_out[g][:, tiles].rearrange("p j h f -> p (j h) f")[:, :, NOPE:],
+                    out=k_heads[g][:, tiles, h, NOPE:],
+                    in_=rope_out[g][:, tiles, :],
                 )
 
         def project_up(step, i):
             if step >= STEPS - 1:
-                kv = psum.tile([P, H, NOPE + VD], F32, name="kv_last", tag="latent", bufs=3)
+                kv = psum.tile([P, H * (NOPE + VD)], F32, name="kv_last", tag="latent", bufs=3)
             else:
-                kv = psum.tile([P, H, NOPE + VD], F32, name="kv", bufs=2)
-            multiply(kv[:].rearrange("p h f -> p (h f)"), step + KVN_LAG, 1, i, wb_codes[:], wb_scales[:])
+                kv = psum.tile([P, H * (NOPE + VD)], F32, name="kv", bufs=2)
+            multiply(kv[:], step + KVN_LAG, 1, i, wb_codes[:], wb_scales[:])
             kv_tiles[step, i] = kv
 
-        def store_k(step, i):
+        def store(step, i):
             g, j = step // STEPS_PER_GROUP, (step % STEPS_PER_GROUP) * STEP_TILES + i
-            nc.scalar.copy(out=k_out[g][:, j, :, 0:NOPE], in_=kv_tiles[step, i][:, :, 0:NOPE])
-            width = NOPE if g >= GROUPS - 2 else NOPE + ROPE
-            nc.sync.dma_start(
-                out=k_groups[g][:, j, :].rearrange("p (h f) -> p h f", h=H)[:, :, 0:width],
-                in_=k_out[g][:, j, :, 0:width],
-            )
-
-        def store_v(step, i):
-            g, j = step // STEPS_PER_GROUP, (step % STEPS_PER_GROUP) * STEP_TILES + i
-            copy = nc.vector.tensor_copy if step >= STEPS - 2 else nc.scalar.copy
-            copy(out=v_out[g][:, j, :, :], in_=kv_tiles[step, i][:, :, NOPE:])
-            nc.sync.dma_start(out=v_groups[g][:, j, :], in_=v_out[g][:, j].rearrange("p h f -> p (h f)"))
+            copy = nc.vector.tensor_copy if i == 1 and step >= STEPS - 2 else nc.scalar.copy
+            copy(out=kv_out[g][:, j].rearrange("p s h f -> p (s h f)"), in_=kv_tiles[step, i][:])
+            nc.sync.dma_start(out=k_heads[g][:, j, :, 0:NOPE], in_=kv_out[g][:, j, 0])
+            nc.sync.dma_start(out=v_groups[g][:, j, :], in_=kv_out[g][:, j, 1].rearrange("p h f -> p (h f)"))
 
         def pipeline_round(rnd):
             entering, down, flipping, up = rnd + X_LEAD, rnd, rnd - KVN_LAG, rnd - KVN_LAG - 1
@@ -339,11 +328,10 @@ def tile_mla_pb_t_kernel(tc, hidden_states, w_kv_a, kv_a_ln_w, w_kv_b, out_0, ou
                     copy_x(entering, nc.scalar.copy)
                 if 0 <= up < STEPS:
                     project_up(up, i)
-                    store_k(up, i)
+                    if not (i == 1 and up >= STEPS - 2):
+                        store(up, i)
                 if 0 <= down < STEPS:
                     invert_rms(down, i)
-                if 0 <= up < STEPS - 2:
-                    store_v(up, i)
             if 0 <= down < STEPS:
                 rotate(down)
             if 0 <= flipping < STEPS:
@@ -354,13 +342,13 @@ def tile_mla_pb_t_kernel(tc, hidden_states, w_kv_a, kv_a_ln_w, w_kv_b, out_0, ou
                     quantise_pair(rnd)
                 normalise(down, 1)
             if STEPS - 2 <= up < STEPS:
-                for i in range(STEP_TILES):
-                    store_v(up, i)
+                store(up, 1)
 
-        def regroup_on_gpsimd(block):
+        def regroup_on_gpsimd(part, h):
+            block, source = (first * P for first in (part * H + h, h * 2 + part))
             nc.gpsimd.tensor_scalar(
-                out=wb_grouped[:, block, :],
-                in0=wb_rows[:, :, block].rearrange("p t c -> p c t"),
+                out=wb_grouped[:, block : block + P, :],
+                in0=wb_rows[:, :, source : source + P].rearrange("p t c -> p c t"),
                 scalar1=1.0,
                 scalar2=0.0,
                 op0=ALU.mult,
@@ -401,11 +389,10 @@ def tile_mla_pb_t_kernel(tc, hidden_states, w_kv_a, kv_a_ln_w, w_kv_b, out_0, ou
         copy_x(1, nc.vector.tensor_copy)
         quantise_weight(wa_grouped, wa_codes, wa_scales, slice(KVL, KVL + ROPE))
         quantise_pair(-1)
-        for block in range(0, 384, 128):
-            regroup_on_gpsimd(slice(block, block + 128))
+        for part, h in ((0, 0), (0, 1), (1, 0)):
+            regroup_on_gpsimd(part, h)
         pipeline_round(0)
-        for block in range(384, 512, 128):
-            regroup_on_gpsimd(slice(block, block + 128))
+        regroup_on_gpsimd(1, 1)
         pipeline_round(1)
         quantise_weight(wb_grouped, wb_codes, wb_scales, slice(0, H * (NOPE + VD)))
         for rnd in range(2, STEPS + KVN_LAG + 1):

import math
from contextlib import ExitStack

import concourse.mybir as mybir
from concourse.masks import make_identity

F32 = mybir.dt.float32
BF16 = mybir.dt.bfloat16
I32 = mybir.dt.int32
U32 = mybir.dt.uint32
U8 = mybir.dt.uint8
FP8X4 = mybir.dt.float8_e4m3fn_x4
ALU = mybir.AluOpType
ACT = mybir.ActivationFunctionType

B, S, D, H, KVL, NOPE, ROPE, VD = 4, 1024, 512, 2, 512, 128, 128, 128
HALF = ROPE // 2
ROPE_BASE = 10000.0
EPS = 1e-6

P = 128
PACK = 4
WORD_HALVES = 2
GROUP_TILES = 4
GROUP_TOKENS = P * GROUP_TILES
GROUPS = B * S // GROUP_TOKENS
SEQ_TILES = S // P
STEP_TILES = 2
STEPS = GROUPS * GROUP_TILES // STEP_TILES
STEPS_PER_GROUP = GROUP_TILES // STEP_TILES
X_LEAD = 2
KVN_LAG = 2
SEED = 16
ROUND_TO_INTEGER = 1.5 * 2.0**23

FLOPS = 2 * B * S * D * (KVL + ROPE) + 2 * B * S * KVL * H * (NOPE + VD)


def tile_mla_pb_t_kernel(tc, hidden_states, w_kv_a, kv_a_ln_w, w_kv_b, out_0, out_1):
    nc = tc.nc

    x_groups = hidden_states.rearrange("b s d -> (b s) d").rearrange(
        "(g p j) d -> g p j d", p=P, j=GROUP_TILES
    )
    k_heads = out_0.rearrange("b s h f -> (b s) h f").rearrange("(g p j) h f -> g p j h f", p=P, j=GROUP_TILES)
    v_groups = out_1.rearrange("b s h f -> (b s) (h f)").rearrange(
        "(g p j) f -> g p j f", p=P, j=GROUP_TILES
    )

    with ExitStack() as ctx:
        consts = ctx.enter_context(tc.tile_pool(name="consts", bufs=1))
        inputs = ctx.enter_context(tc.tile_pool(name="inputs", bufs=GROUPS))
        work = ctx.enter_context(tc.tile_pool(name="work", bufs=3))
        results = ctx.enter_context(tc.tile_pool(name="results", bufs=GROUPS))
        psum = ctx.enter_context(tc.psum_pool(name="psum", bufs=1))
        ctx.enter_context(tc.manual_schedule())

        def load_weight(w, columns, name):
            rows = consts.tile([P, PACK, columns], BF16, name=name)
            nc.sync.dma_start(
                out=rows[:].rearrange("p (u e) c -> p u (e c)", e=2),
                in_=w.rearrange("(u p e) c -> p u (e c)", u=WORD_HALVES, e=2),
            )
            return rows

        x_tiles = [inputs.tile([P, GROUP_TILES, D], BF16, name="x_sb") for g in range(GROUPS)]

        def load_x(g, first, count):
            tiles = slice(first, first + count)
            nc.sync.dma_start(out=x_tiles[g][:, tiles, :], in_=x_groups[g][:, tiles, :])

        load_x(0, 0, STEP_TILES)
        wa_rows = load_weight(w_kv_a, KVL + ROPE, "wa_rows")
        gain_row = consts.tile([P, KVL], BF16)
        nc.gpsimd.memset(gain_row[:], 0.0)
        nc.sync.dma_start(out=gain_row[0:1, :], in_=kv_a_ln_w.unsqueeze(0))
        load_x(0, STEP_TILES, STEP_TILES)
        wb_rows = load_weight(w_kv_b, H * (NOPE + VD), "wb_rows")
        for g in range(1, GROUPS):
            load_x(g, 0, GROUP_TILES)

        table_warmer = consts.tile([P, 1], F32)
        eps = consts.tile([P, 1], F32)
        nc.gpsimd.memset(eps[:], EPS)
        ones = consts.tile([P, P], BF16)
        nc.gpsimd.memset(ones[:], 1.0)

        position = consts.tile([P, SEQ_TILES], F32)
        nc.gpsimd.iota(
            position[:],
            pattern=[[GROUP_TOKENS, SEQ_TILES // GROUP_TILES], [1, GROUP_TILES]],
            base=0,
            channel_multiplier=GROUP_TILES,
            allow_small_or_imprecise_dtypes=True,
        )
        identity = consts.tile([P, P], F32)
        make_identity(nc, identity[:])
        seed = consts.tile([P, SEED], F32)
        nc.vector.memset(seed[:, 0:1], 1.0)
        done = 1
        while done < SEED:
            nc.vector.tensor_scalar_mul(
                out=seed[:, done : 2 * done], in0=seed[:, 0:done], scalar1=ROPE_BASE ** (-done / HALF)
            )
            done *= 2
        turns = consts.tile([P, SEQ_TILES, HALF], F32)
        nc.vector.scalar_tensor_tensor(
            out=turns[:, :, 0:SEED],
            in0=seed[:].unsqueeze(1).to_broadcast([P, SEQ_TILES, SEED]),
            scalar=1.0 / (2.0 * math.pi),
            in1=position[:].unsqueeze(2).to_broadcast([P, SEQ_TILES, SEED]),
            op0=ALU.mult,
            op1=ALU.mult,
        )
        for first in range(SEED, HALF, SEED):
            nc.vector.tensor_scalar_mul(
                out=turns[:, :, first : first + SEED],
                in0=turns[:, :, 0:SEED],
                scalar1=ROPE_BASE ** (-first / HALF),
            )
        halves = [slice(first, first + GROUP_TILES) for first in range(0, SEQ_TILES, GROUP_TILES)]
        nearest = consts.tile([P, SEQ_TILES, HALF], F32)
        fraction = consts.tile([P, SEQ_TILES, HALF], F32)
        size = consts.tile([P, SEQ_TILES, HALF], F32)
        for entries in halves:
            nc.vector.tensor_scalar(
                out=nearest[:, entries],
                in0=turns[:, entries],
                scalar1=ROUND_TO_INTEGER,
                scalar2=ROUND_TO_INTEGER,
                op0=ALU.add,
                op1=ALU.subtract,
            )
        for entries in halves:
            nc.vector.tensor_tensor(
                out=fraction[:, entries], in0=turns[:, entries], in1=nearest[:, entries], op=ALU.subtract
            )
        def new_weight(columns, name):
            return (
                consts.tile([P, columns, PACK], BF16, name=name + "_grouped", align_bytes=64),
                consts.tile([P, columns], U32, name=name + "_codes", align_bytes=64),
                consts.tile([P, columns], U8, name=name + "_scales", align_bytes=64),
            )

        def regroup_weight(rows, grouped, block):
            nc.vector.tensor_copy(
                out=grouped[:, block, :].rearrange("p (c i) t -> p c t i", i=PACK),
                in_=rows[:, :, block].rearrange("p t (c i) -> p c t i", i=PACK),
            )

        def quantise_weight(grouped, codes, scales, block):
            nc.vector.quantize_mx(
                out=codes[:, block].bitcast(FP8X4),
                scales=scales[:, block],
                in_=grouped[:, block, :].rearrange("p c t -> p (c t)"),
            )

        wa_grouped, wa_codes, wa_scales = new_weight(KVL + ROPE, "wa")
        wb_grouped, wb_codes, wb_scales = new_weight(H * (NOPE + VD), "wb")
        x_flipped, kvn_rows = {}, {}
        grouped, codes, scales = {}, {}, {}
        k_pe, mean_square, inverse_rms, latents = {}, {}, {}, {}
        kv_tiles, kv_out, rope_out = {}, {}, {}

        def transpose_words(rows_bf16, name):
            words = rows_bf16.bitcast(F32)
            flipped = psum.tile([P, STEP_TILES, WORD_HALVES, P], F32, name=name, tag="flipped", bufs=2)
            for i in range(STEP_TILES):
                for u in range(WORD_HALVES):
                    nc.tensor.transpose(flipped[:, i, u, :], words[:, i, u * P : (u + 1) * P], identity[:])
            return flipped

        def new_pair(rnd):
            grouped[rnd] = work.tile([P, 2, STEP_TILES, P, PACK], BF16, name="grouped", align_bytes=64, bufs=STEPS // 2)
            codes[rnd] = work.tile([P, 2, STEP_TILES * P], U32, name="codes", align_bytes=64, bufs=4)
            scales[rnd] = work.tile([P, 2, STEP_TILES * P], U8, name="scales", align_bytes=64, bufs=4)

        def quantise_pair(rnd):
            kinds = slice(0 if rnd + X_LEAD < STEPS else 1, 2 if rnd >= KVN_LAG else 1)
            nc.vector.quantize_mx(
                out=codes[rnd][:, kinds, :].rearrange("p k c -> p (k c)").bitcast(FP8X4),
                scales=scales[rnd][:, kinds, :].rearrange("p k c -> p (k c)"),
                in_=grouped[rnd][:, kinds].rearrange("p k i t w -> p (k i t w)"),
            )

        def multiply(out, pair, kind, i, weight_codes, weight_scales):
            tokens = slice(i * P, (i + 1) * P)
            nc.tensor.matmul_mx(
                out=out,
                lhsT=codes[pair][:, kind, tokens].bitcast(FP8X4),
                lhsT_scale=scales[pair][:, kind, tokens],
                rhs=weight_codes.bitcast(FP8X4),
                rhs_scale=weight_scales,
                start=True,
                stop=True,
            )

        def flip_x(step):
            g, first_tile = step // STEPS_PER_GROUP, (step % STEPS_PER_GROUP) * STEP_TILES
            x_flipped[step] = transpose_words(x_tiles[g][:, first_tile : first_tile + STEP_TILES, :], "x_words")

        def copy_x(step, copy):
            copy(
                out=grouped[step - X_LEAD][:, 0].bitcast(F32), in_=x_flipped[step][:].rearrange("p i u t -> p i t u")
            )

        def flip_kvn(step):
            flipped = transpose_words(kvn_rows[step][:], "kvn_flipped")
            copy = nc.scalar.copy if step in (0, STEPS - 2) else nc.vector.tensor_copy
            copy(
                out=grouped[step + KVN_LAG][:, 1].bitcast(F32), in_=flipped[:].rearrange("p i u t -> p i t u")
            )

        def spread_gain():
            spread = psum.tile([P, KVL], BF16, name="spread", tag="latent", bufs=3)
            nc.tensor.matmul(out=spread[:], lhsT=ones[:], rhs=gain_row[:], start=True, stop=True)
            gain = consts.tile([P, KVL], BF16, name="gain")
            nc.vector.tensor_copy(out=gain[:], in_=spread[:])
            return gain

        def project_down(step, i):
            if i == 0:
                k_pe[step] = psum.tile([P, STEP_TILES, ROPE], F32, name="k_pe")
                mean_square[step] = work.tile([P, STEP_TILES], F32, name="mean_square")
                inverse_rms[step] = work.tile([P, STEP_TILES], F32, name="inverse_rms", bufs=STEPS)
                latents[step] = []
            latent = psum.tile([P, KVL], F32, name="latent", tag="latent", bufs=3)
            multiply(latent[:], step - X_LEAD, 0, i, wa_codes[:, 0:KVL], wa_scales[:, 0:KVL])
            latents[step].append(latent)
            if i == STEP_TILES - 1:
                columns = slice(KVL, KVL + ROPE)
                for tile in range(STEP_TILES):
                    multiply(
                        k_pe[step][:, tile, :], step - X_LEAD, 0, tile, wa_codes[:, columns], wa_scales[:, columns]
                    )

        def square(step, i):
            squares = work.tile([P, KVL], BF16, name="squares")
            nc.scalar.activation(
                out=squares[:],
                in_=latents[step][i][:],
                func=ACT.Square,
                scale=KVL**-0.5,
                accum_out=mean_square[step][:, i : i + 1],
            )

        def invert_rms(step, i):
            nc.scalar.activation(
                out=inverse_rms[step][:, i : i + 1],
                in_=mean_square[step][:, i : i + 1],
                func=ACT.Abs_reciprocal_sqrt,
                bias=eps[:],
                scale=1.0,
            )

        def normalise(step, i):
            if i == 0:
                kvn_rows[step] = work.tile([P, STEP_TILES, KVL], BF16, name="kvn_rows")
            nc.vector.scalar_tensor_tensor(
                out=kvn_rows[step][:, i, :],
                in0=latents[step][i][:],
                scalar=inverse_rms[step][:, i : i + 1],
                in1=gain[:],
                op0=ALU.mult,
                op1=ALU.mult,
            )

        def rotate(step):
            g, first_tile = step // STEPS_PER_GROUP, (step % STEPS_PER_GROUP) * STEP_TILES
            if first_tile == 0:
                kv_out[g] = results.tile([P, GROUP_TILES, 2, H, P], F32, name="kv_out")
                rope_out[g] = results.tile([P, GROUP_TILES, ROPE], F32, name="rope_out")
            first_entry = (g % (SEQ_TILES // GROUP_TILES)) * GROUP_TILES + first_tile
            entries = slice(first_entry, first_entry + STEP_TILES)
            shape = [P, STEP_TILES, 2, 2, HALF]
            products = work.tile([P, STEP_TILES, 2, ROPE], F32, name="products", bufs=STEPS)
            nc.vector.tensor_tensor(
                out=products[:].rearrange("p j s (h i) -> p j s h i", h=2),
                in0=k_pe[step][:].rearrange("p j (h i) -> p j h i", h=2).unsqueeze(2).to_broadcast(shape),
                in1=factors[:, entries].unsqueeze(3).to_broadcast(shape),
                op=ALU.mult,
            )
            tiles = slice(first_tile, first_tile + STEP_TILES)
            for half in range(2):
                here, there = slice(half * HALF, (half + 1) * HALF), slice((1 - half) * HALF, (2 - half) * HALF)
                nc.gpsimd.tensor_tensor(
                    out=rope_out[g][:, tiles, here],
                    in0=products[:, :, 0, here],
                    in1=products[:, :, 1, there],
                    op=ALU.subtract if half == 0 else ALU.add,
                )
            for h in range(H):
                nc.sync.dma_start(
                    out=k_heads[g][:, tiles, h, NOPE:],
                    in_=rope_out[g][:, tiles, :],
                )

        def project_up(step, i):
            if step >= STEPS - 1:
                kv = psum.tile([P, H * (NOPE + VD)], F32, name="kv_last", tag="latent", bufs=3)
            else:
                kv = psum.tile([P, H * (NOPE + VD)], F32, name="kv", bufs=2)
            multiply(kv[:], step + KVN_LAG, 1, i, wb_codes[:], wb_scales[:])
            kv_tiles[step, i] = kv

        def store(step, i):
            g, j = step // STEPS_PER_GROUP, (step % STEPS_PER_GROUP) * STEP_TILES + i
            copy = nc.vector.tensor_copy if i == 1 and step >= STEPS - 2 else nc.scalar.copy
            copy(out=kv_out[g][:, j].rearrange("p s h f -> p (s h f)"), in_=kv_tiles[step, i][:])
            nc.sync.dma_start(out=k_heads[g][:, j, :, 0:NOPE], in_=kv_out[g][:, j, 0])
            nc.sync.dma_start(out=v_groups[g][:, j, :], in_=kv_out[g][:, j, 1].rearrange("p h f -> p (h f)"))

        def pipeline_round(rnd):
            entering, down, flipping, up = rnd + X_LEAD, rnd, rnd - KVN_LAG, rnd - KVN_LAG - 1
            filling = flipping < 0
            new_pair(rnd)
            if 0 <= entering < STEPS and not filling:
                flip_x(entering)
                copy_x(entering, nc.scalar.copy)
            if 0 <= flipping < STEPS:
                flip_kvn(flipping)
            for i in range(STEP_TILES):
                if 0 <= down < STEPS:
                    project_down(down, i)
                    square(down, i)
                if filling and i == 0:
                    flip_x(entering)
                    copy_x(entering, nc.scalar.copy)
                if 0 <= up < STEPS:
                    project_up(up, i)
                    if not (i == 1 and up >= STEPS - 2):
                        store(up, i)
                if 0 <= down < STEPS:
                    invert_rms(down, i)
            if 0 <= down < STEPS:
                rotate(down)
            if 0 <= flipping < STEPS:
                quantise_pair(rnd)
            if 0 <= down < STEPS:
                normalise(down, 0)
                if filling:
                    quantise_pair(rnd)
                normalise(down, 1)
            if STEPS - 2 <= up < STEPS:
                store(up, 1)

        def regroup_on_gpsimd(part, h):
            block, source = (first * P for first in (part * H + h, h * 2 + part))
            nc.gpsimd.tensor_scalar(
                out=wb_grouped[:, block : block + P, :],
                in0=wb_rows[:, :, source : source + P].rearrange("p t c -> p c t"),
                scalar1=1.0,
                scalar2=0.0,
                op0=ALU.mult,
                op1=ALU.add,
            )

        new_pair(-2)
        flip_x(0)
        nc.scalar.activation(out=table_warmer[:], in_=eps[:], func=ACT.Sin)
        copy_x(0, nc.scalar.copy)
        factors = consts.tile([P, SEQ_TILES, 2, HALF], F32)
        for entries in halves:
            nc.scalar.activation(
                out=factors[:, entries, 1, :], in_=fraction[:, entries], func=ACT.Sin, scale=2.0 * math.pi
            )
        for entries in halves:
            nc.scalar.activation(out=size[:, entries], in_=fraction[:, entries], func=ACT.Abs)
        for entries in halves:
            nc.scalar.activation(
                out=factors[:, entries, 0, :],
                in_=size[:, entries],
                func=ACT.Sin,
                scale=-2.0 * math.pi,
                bias=0.5 * math.pi,
            )

        latent_halves = [slice(0, KVL // 2), slice(KVL // 2, KVL)]
        regroup_weight(wa_rows, wa_grouped, latent_halves[0])
        quantise_pair(-2)
        regroup_weight(wa_rows, wa_grouped, latent_halves[1])
        for block in latent_halves:
            quantise_weight(wa_grouped, wa_codes, wa_scales, block)
        gain = spread_gain()
        nc.scalar.activation(out=table_warmer[:], in_=eps[:], func=ACT.Abs_reciprocal_sqrt)
        new_pair(-1)
        flip_x(1)
        regroup_weight(wa_rows, wa_grouped, slice(KVL, KVL + ROPE))
        copy_x(1, nc.vector.tensor_copy)
        quantise_weight(wa_grouped, wa_codes, wa_scales, slice(KVL, KVL + ROPE))
        quantise_pair(-1)
        for part, h in ((0, 0), (0, 1), (1, 0)):
            regroup_on_gpsimd(part, h)
        pipeline_round(0)
        regroup_on_gpsimd(1, 1)
        pipeline_round(1)
        quantise_weight(wb_grouped, wb_codes, wb_scales, slice(0, H * (NOPE + VD)))
        for rnd in range(2, STEPS + KVN_LAG + 1):
            pipeline_round(rnd)
